import numpy as np
import ml_dtypes


def mxq(x, axis, fmt="e4m3"):
    dtype, down = {"e4m3": (ml_dtypes.float8_e4m3fn, 7), "e5m2": (ml_dtypes.float8_e5m2, 14)}[fmt]
    v = np.moveaxis(np.asarray(x, np.float32).astype(ml_dtypes.bfloat16).astype(np.float64), axis, -1)
    blocks = v.reshape(v.shape[:-1] + (-1, 32))
    amax = np.abs(blocks).max(-1, keepdims=True)
    byte = np.maximum(np.where(amax > 0, np.frexp(amax)[1] - 1 + 127, 0) - down, 1)
    scale = np.exp2(byte - 127.0)
    codes = (blocks / scale).astype(np.float32).astype(dtype).astype(np.float64)
    return np.moveaxis((codes * scale).reshape(v.shape), -1, axis)


WIDE = False


def mx_kscale(k):
    if not WIDE:
        return np.ones(k)
    levels = np.array([10, -10, 5, -5, 0])
    a = np.random.permutation(np.resize(levels, k // 512 * 4)).reshape(k // 512, 4)
    idx = np.arange(k)
    return np.exp2(a[idx // 512, idx % 128 // 32])


BF16 = ml_dtypes.bfloat16


def bf(x):
    return np.asarray(x, np.float32).astype(BF16)


def f64(x):
    return np.asarray(x).astype(np.float64)


B, IN, E1, E2, LAT, D1, D2 = 4096, 512, 1536, 1024, 256, 512, 512


def silu(v):
    return v / (1.0 + np.exp(-v))


def softplus(v):
    return np.maximum(v, 0.0) + np.log(1.0 + np.exp(-np.abs(v)))


def sigmoid(v):
    return 1.0 / (1.0 + np.exp(-v))


def setup_inputs():
    s = mx_kscale(D1)
    return {
        'h_dec0': bf(silu(np.random.standard_normal((B, D1)) * 1.3) * s),
        'x': bf(np.random.uniform(0.0, 1.0, (B, IN))),
        'dw1': bf(np.random.standard_normal((D1, D2)) * 1.3 / np.sqrt(D1) / s[:, None]),
        'db1': bf(np.random.standard_normal(D2) * 0.3),
        'dw2': bf(np.random.standard_normal((D2, IN)) * 1.6 / np.sqrt(D2)),
        'db2': bf(np.random.standard_normal(IN) * 0.3 - 0.5),
    }


def reference(h_dec0, x, dw1, db1, dw2, db2):
    h = silu((mxq(f64(h_dec0), 1, 'e4m3') @ mxq(f64(dw1), 0, 'e4m3')) + f64(db1))
    logits = (mxq(h, 1, 'e4m3') @ mxq(f64(dw2), 0, 'e4m3')) + f64(db2)
    bce = np.maximum(logits, 0.0) - logits * f64(x) + softplus(-np.abs(logits))
    return bce.sum(-1), sigmoid(logits)

@@ -1,0 +1,275 @@
+from contextlib import ExitStack
+
+import concourse.mybir as mybir
+from concourse.masks import make_identity
+
+F32 = mybir.dt.float32
+BF16 = mybir.dt.bfloat16
+U32 = mybir.dt.uint32
+U8 = mybir.dt.uint8
+FP8X4 = mybir.dt.float8_e4m3fn_x4
+ACT = mybir.ActivationFunctionType
+ALU = mybir.AluOpType
+
+P = 128
+BATCH = 4096
+WIDTH = 512
+FLOPS = 2 * 2 * BATCH * WIDTH * WIDTH
+ROWS = BATCH // P
+TILES = 4
+CHUNKS = ROWS // TILES
+CW = TILES * WIDTH
+CLAMP = -40.0
+GROUPS = 2
+EARLY = 2
+
+
+def tile_vae_pb_t_kernel(tc, h_dec0, x, dw1, db1, dw2, db2, out_0, out_1):
+    nc = tc.nc
+    h_rows = h_dec0.rearrange("(p q) k -> p (q k)", q=ROWS)
+    x_rows = x.rearrange("(p q) k -> p (q k)", q=ROWS)
+    o_rows = out_1.rearrange("(p q) k -> p (q k)", q=ROWS)
+
+    with ExitStack() as ctx:
+        const = ctx.enter_context(tc.tile_pool(name="const", bufs=1))
+        io = ctx.enter_context(tc.tile_pool(name="io", bufs=CHUNKS))
+        work = ctx.enter_context(tc.tile_pool(name="work", bufs=2))
+        ps_t = ctx.enter_context(tc.psum_pool(name="ps_t", bufs=2))
+        ps_z = ctx.enter_context(tc.psum_pool(name="ps_z", bufs=4))
+        ps_a = ctx.enter_context(tc.psum_pool(name="ps_a", bufs=2))
+        ctx.enter_context(tc.manual_schedule())
+
+        ident = const.tile([P, P], F32, name="ident")
+        w1c = const.tile([P, WIDTH], U32, name="w1c", align_bytes=64)
+        w1s = const.tile([P, WIDTH], U8, name="w1s", align_bytes=64)
+        w2c = const.tile([P, WIDTH], U32, name="w2c", align_bytes=64)
+        w2s = const.tile([P, WIDTH], U8, name="w2s", align_bytes=64)
+        b1r = const.tile([P, 4], BF16, name="b1r")
+        b1f = const.tile([P, 4], F32, name="b1f")
+        b2bc = const.tile([P, WIDTH], BF16, name="b2bc")
+        sum_lc = const.tile([P, ROWS], F32, name="sum_lc")
+        sum_lx = const.tile([P, ROWS], F32, name="sum_lx")
+        sum_ln = const.tile([P, ROWS], F32, name="sum_ln")
+        part = const.tile([P, ROWS], F32, name="part")
+        bce = const.tile([P, ROWS], F32, name="bce")
+        junk = const.tile([P, WIDTH], BF16, name="junk")
+        logit = [const.tile([P, TILES, WIDTH], F32, name="logit%d" % c) for c in range(CHUNKS)]
+        recon = [const.tile([P, TILES, WIDTH], F32, name="recon%d" % c) for c in range(CHUNKS)]
+        c1 = [const.tile([P, WIDTH], U32, name="c1_%d" % c, align_bytes=64) for c in range(CHUNKS)]
+        s1 = [const.tile([P, WIDTH], U8, name="s1_%d" % c, align_bytes=64) for c in range(CHUNKS)]
+
+        h0 = {}
+        xs = {}
+        xts = {}
+        g0 = {}
+        c0 = {}
+        s0 = {}
+        zs = {}
+        hs = {}
+        g1 = {}
+        accs = {}
+
+        def load_h(c):
+            h0[c] = io.tile([P, CW], BF16, name="h0_%d" % c, tag="io")
+            nc.sync.dma_start(out=h0[c][:], in_=h_rows[:, CW * c : CW * (c + 1)])
+
+        def load_x(c):
+            xs[c] = io.tile([P, CW], BF16, name="x_%d" % c, tag="io")
+            nc.sync.dma_start(out=xs[c][:], in_=x_rows[:, CW * c : CW * (c + 1)])
+
+        def transposes(c):
+            words = h0[c][:].bitcast(F32)
+            for b in range(2):
+                xt = ps_t.tile([P, 2, 256], F32, name="xt%d_%d" % (c, b), tag="xt")
+                for r2 in range(2):
+                    for u in range(2):
+                        lo = 256 * (2 * b + r2) + P * u
+                        nc.tensor.transpose(xt[:, u, P * r2 : P * (r2 + 1)], words[:, lo : lo + P], ident[:])
+                xts[(c, b)] = xt
+
+        def evacuate(c):
+            g0[c] = work.tile([P, CW], BF16, name="g0_%d" % c, tag="g0", align_bytes=64)
+            pairs = g0[c][:].bitcast(F32).rearrange("p (w u) -> p w u", u=2)
+            for b in range(2):
+                nc.scalar.copy(
+                    out=pairs[:, 256 * b : 256 * (b + 1), :],
+                    in_=xts[(c, b)][:].rearrange("p u w -> p w u"),
+                )
+
+        def quantise0(c):
+            c0[c] = work.tile([P, WIDTH], U32, name="c0_%d" % c, tag="c0", align_bytes=64)
+            s0[c] = work.tile([P, WIDTH], U8, name="s0_%d" % c, tag="s0", align_bytes=64)
+            nc.vector.quantize_mx(out=c0[c][:].bitcast(FP8X4), scales=s0[c][:], in_=g0[c][:])
+
+        def layer1(c):
+            for t in range(4):
+                z = ps_z.tile([P, WIDTH], F32, name="z%d_%d" % (c, t), tag="z")
+                nc.tensor.matmul_mx(
+                    out=z[:],
+                    lhsT=w1c[:, P * t : P * (t + 1)].bitcast(FP8X4),
+                    lhsT_scale=w1s[:, P * t : P * (t + 1)],
+                    rhs=c0[c][:].bitcast(FP8X4),
+                    rhs_scale=s0[c][:],
+                    start=True,
+                    stop=True,
+                )
+                zs[(c, t)] = z
+
+        def silu(c):
+            hs[c] = work.tile([P, 4, WIDTH], BF16, name="hs%d" % c, tag="hs")
+            for t in range(4):
+                nc.scalar.activation(
+                    out=hs[c][:, t, :], in_=zs[(c, t)][:], func=ACT.Silu, bias=b1f[:, t : t + 1], scale=1.0
+                )
+
+        def regroup(c):
+            g1[c] = work.tile([P, WIDTH, 4], BF16, name="g1_%d" % c, tag="g1", align_bytes=64)
+            nc.vector.tensor_copy(
+                out=g1[c][:].rearrange("p (c i) t -> p c t i", i=4),
+                in_=hs[c][:].rearrange("p t (c i) -> p c t i", i=4),
+            )
+
+        def quantise1(c):
+            nc.vector.quantize_mx(
+                out=c1[c][:].bitcast(FP8X4), scales=s1[c][:], in_=g1[c][:].rearrange("p w t -> p (w t)")
+            )
+
+        def layer2(j):
+            if j >= ROWS:
+                return
+            c, r = divmod(j, TILES)
+            acc = ps_a.tile([P, WIDTH], F32, name="acc%d" % j, tag="acc")
+            nc.tensor.matmul_mx(
+                out=acc[:],
+                lhsT=c1[c][:, P * r : P * (r + 1)].bitcast(FP8X4),
+                lhsT_scale=s1[c][:, P * r : P * (r + 1)],
+                rhs=w2c[:].bitcast(FP8X4),
+                rhs_scale=w2s[:],
+                start=True,
+                stop=True,
+            )
+            accs[j] = acc
+
+        def add_bias(j):
+            c, r = divmod(j, TILES)
+            nc.vector.tensor_tensor(out=logit[c][:, r, :], in0=accs[j][:], in1=b2bc[:], op=ALU.add)
+
+        def clamp(j):
+            c, r = divmod(j, TILES)
+            nc.vector.tensor_scalar(
+                out=recon[c][:, r, :],
+                in0=logit[c][:, r, :],
+                scalar1=CLAMP,
+                scalar2=None,
+                op0=ALU.max,
+                op1=ALU.add,
+                accum_out=sum_lc[:, j : j + 1],
+            )
+
+        def sigmoid_store(c):
+            flat = recon[c][:].rearrange("p r k -> p (r k)")
+            nc.scalar.activation(out=flat, in_=flat, func=ACT.Sigmoid)
+            nc.sync.dma_start(out=o_rows[:, CW * c : CW * (c + 1)], in_=flat)
+
+        def log_sum(c):
+            for r in range(TILES):
+                j = TILES * c + r
+                nc.scalar.activation(out=junk[:], in_=recon[c][:, r, :], func=ACT.Ln, accum_out=sum_ln[:, j : j + 1])
+
+        def dot_x(c):
+            for r in range(TILES):
+                j = TILES * c + r
+                nc.vector.scalar_tensor_tensor(
+                    out=logit[c][:, r, :],
+                    in0=logit[c][:, r, :],
+                    scalar=1.0,
+                    in1=xs[c][:, WIDTH * r : WIDTH * (r + 1)],
+                    op0=ALU.mult,
+                    op1=ALU.mult,
+                    accum_out=sum_lx[:, j : j + 1],
+                )
+
+        make_identity(nc, ident[:])
+        nc.sync.dma_start(out=b1r[:], in_=db1.rearrange("(p t) -> p t", t=4))
+        raw1 = work.tile([P, CW], BF16, name="raw1", tag="hs")
+        nc.sync.dma_start(
+            out=raw1[:].rearrange("p (u f) -> p u f", u=2),
+            in_=dw1.rearrange("(u p e) n -> p u (e n)", u=2, p=P, e=2),
+        )
+        load_h(0)
+        load_h(1)
+        raw2 = work.tile([P, CW], BF16, name="raw2", tag="hs")
+        nc.sync.dma_start(out=raw2[:], in_=dw2.rearrange("(p t) n -> p (t n)", t=4))
+        nc.sync.dma_start(out=b2bc[:], in_=db2.partition_broadcast(P))
+        for c in range(2, CHUNKS):
+            load_h(c)
+
+        nc.vector.tensor_copy(out=b1f[:], in_=b1r[:])
+        wg1 = work.tile([P, CW], BF16, name="wg1", tag="g1", align_bytes=64)
+        nc.vector.tensor_copy(
+            out=wg1[:].rearrange("p (s m t) -> p s m t", s=4, m=P, t=4),
+            in_=raw1[:].rearrange("p (t m s) -> p s m t", t=4, m=P, s=4),
+        )
+        nc.vector.quantize_mx(out=w1c[:].bitcast(FP8X4), scales=w1s[:], in_=wg1[:])
+
+        transposes(0)
+        evacuate(0)
+        transposes(1)
+        evacuate(1)
+        quantise0(0)
+        wg2 = work.tile([P, CW], BF16, name="wg2", tag="g1", align_bytes=64)
+        nc.vector.tensor_copy(
+            out=wg2[:].rearrange("p (c i t) -> p c t i", i=4, t=4),
+            in_=raw2[:].rearrange("p (t c i) -> p c t i", t=4, i=4),
+        )
+        quantise0(1)
+        nc.vector.quantize_mx(out=w2c[:].bitcast(FP8X4), scales=w2s[:], in_=wg2[:])
+        layer1(0)
+
+        def epilogue_step(j):
+            if j < ROWS:
+                add_bias(j)
+            if j >= 1:
+                clamp(j - 1)
+
+        for c in range(CHUNKS):
+            silu(c)
+            if c + 2 < CHUNKS:
+                transposes(c + 2)
+                evacuate(c + 2)
+            load_x(c)
+            if c + 1 < CHUNKS:
+                layer1(c + 1)
+            if c >= 2:
+                for e in range(EARLY):
+                    layer2(EARLY * (c - 2) + e + 2)
+            regroup(c)
+            if c + 2 < CHUNKS:
+                quantise0(c + 2)
+            quantise1(c)
+            if c == 0:
+                layer2(0)
+                layer2(1)
+            else:
+                for e in range(EARLY):
+                    epilogue_step(EARLY * (c - 1) + e)
+
+        per_group = CHUNKS // GROUPS
+        finished = []
+        for e in range(EARLY):
+            layer2(EARLY * (CHUNKS - 2) + e + 2)
+        for j in range(EARLY * (CHUNKS - 1), ROWS + 1):
+            epilogue_step(j)
+            layer2(j + 2)
+            for c in range(len(finished), j // TILES):
+                sigmoid_store(c)
+                finished.append(c)
+                if len(finished) % per_group == 0:
+                    for d in finished[-per_group:]:
+                        log_sum(d)
+        for c in range(CHUNKS):
+            dot_x(c)
+
+        nc.vector.tensor_tensor(out=part[:], in0=sum_lc[:], in1=sum_lx[:], op=ALU.subtract)
+        nc.vector.tensor_tensor(out=bce[:], in0=part[:], in1=sum_ln[:], op=ALU.subtract)
+        nc.sync.dma_start(out=out_0.rearrange("(p q) -> p q", q=ROWS), in_=bce[:])

@@ -22,6 +22,9 @@ CW = TILES * WIDTH
 CLAMP = -40.0
 GROUPS = 2
 EARLY = 2
+LOOK = 3
+DEEP = 8
+FIRST_LATE = EARLY * (CHUNKS - 1)
 
 
 def tile_vae_pb_t_kernel(tc, h_dec0, x, dw1, db1, dw2, db2, out_0, out_1):
@@ -46,7 +49,9 @@ def tile_vae_pb_t_kernel(tc, h_dec0, x, dw1, db1, dw2, db2, out_0, out_1):
         w2s = const.tile([P, WIDTH], U8, name="w2s", align_bytes=64)
         b1r = const.tile([P, 4], BF16, name="b1r")
         b1f = const.tile([P, 4], F32, name="b1f")
-        b2bc = const.tile([P, WIDTH], BF16, name="b2bc")
+        b2bc = const.tile([P, WIDTH], F32, name="b2bc")
+        ones = const.tile([P, P], BF16, name="ones")
+        brow = const.tile([P, WIDTH], BF16, name="brow")
         sum_lc = const.tile([P, ROWS], F32, name="sum_lc")
         sum_lx = const.tile([P, ROWS], F32, name="sum_lx")
         sum_ln = const.tile([P, ROWS], F32, name="sum_ln")
@@ -71,7 +76,12 @@ def tile_vae_pb_t_kernel(tc, h_dec0, x, dw1, db1, dw2, db2, out_0, out_1):
 
         def load_h(c):
             h0[c] = io.tile([P, CW], BF16, name="h0_%d" % c, tag="io")
-            nc.sync.dma_start(out=h0[c][:], in_=h_rows[:, CW * c : CW * (c + 1)])
+            pieces = 2 if c == 0 else 1
+            step = CW // pieces
+            for i in range(pieces):
+                nc.sync.dma_start(
+                    out=h0[c][:, step * i : step * (i + 1)], in_=h_rows[:, CW * c + step * i : CW * c + step * (i + 1)]
+                )
 
         def load_x(c):
             xs[c] = io.tile([P, CW], BF16, name="x_%d" % c, tag="io")
@@ -88,7 +98,7 @@ def tile_vae_pb_t_kernel(tc, h_dec0, x, dw1, db1, dw2, db2, out_0, out_1):
                 xts[(c, b)] = xt
 
         def evacuate(c):
-            g0[c] = work.tile([P, CW], BF16, name="g0_%d" % c, tag="g0", align_bytes=64)
+            g0[c] = work.tile([P, CW], BF16, name="g0_%d" % c, tag="g0", bufs=LOOK, align_bytes=64)
             pairs = g0[c][:].bitcast(F32).rearrange("p (w u) -> p w u", u=2)
             for b in range(2):
                 nc.scalar.copy(
@@ -97,8 +107,8 @@ def tile_vae_pb_t_kernel(tc, h_dec0, x, dw1, db1, dw2, db2, out_0, out_1):
                 )
 
         def quantise0(c):
-            c0[c] = work.tile([P, WIDTH], U32, name="c0_%d" % c, tag="c0", align_bytes=64)
-            s0[c] = work.tile([P, WIDTH], U8, name="s0_%d" % c, tag="s0", align_bytes=64)
+            c0[c] = work.tile([P, WIDTH], U32, name="c0_%d" % c, tag="c0", bufs=LOOK, align_bytes=64)
+            s0[c] = work.tile([P, WIDTH], U8, name="s0_%d" % c, tag="s0", bufs=LOOK, align_bytes=64)
             nc.vector.quantize_mx(out=c0[c][:].bitcast(FP8X4), scales=s0[c][:], in_=g0[c][:])
 
         def layer1(c):
@@ -138,7 +148,13 @@ def tile_vae_pb_t_kernel(tc, h_dec0, x, dw1, db1, dw2, db2, out_0, out_1):
             if j >= ROWS:
                 return
             c, r = divmod(j, TILES)
-            acc = ps_a.tile([P, WIDTH], F32, name="acc%d" % j, tag="acc")
+            late = (j - FIRST_LATE) % DEEP if j >= FIRST_LATE else 0
+            if late < 2:
+                acc = ps_a.tile([P, WIDTH], F32, name="acc%d" % j, tag="acc")
+            elif late < 6:
+                acc = ps_z.tile([P, WIDTH], F32, name="acc%d" % j, tag="z")
+            else:
+                acc = ps_t.tile([P, WIDTH], F32, name="acc%d" % j, tag="xt")
             nc.tensor.matmul_mx(
                 out=acc[:],
                 lhsT=c1[c][:, P * r : P * (r + 1)].bitcast(FP8X4),
@@ -189,18 +205,20 @@ def tile_vae_pb_t_kernel(tc, h_dec0, x, dw1, db1, dw2, db2, out_0, out_1):
                     accum_out=sum_lx[:, j : j + 1],
                 )
 
+        nc.scalar.dma_start(out=b1r[:], in_=db1.rearrange("(p t) -> p t", t=4))
+        nc.gpsimd.memset(brow[:], 0.0)
+        nc.gpsimd.memset(ones[:], 1.0)
         make_identity(nc, ident[:])
-        nc.sync.dma_start(out=b1r[:], in_=db1.rearrange("(p t) -> p t", t=4))
+        nc.scalar.dma_start(out=brow[0:1, :], in_=db2.rearrange("(o n) -> o n", o=1))
+        load_h(0)
         raw1 = work.tile([P, CW], BF16, name="raw1", tag="hs")
         nc.sync.dma_start(
             out=raw1[:].rearrange("p (u f) -> p u f", u=2),
             in_=dw1.rearrange("(u p e) n -> p u (e n)", u=2, p=P, e=2),
         )
-        load_h(0)
         load_h(1)
         raw2 = work.tile([P, CW], BF16, name="raw2", tag="hs")
         nc.sync.dma_start(out=raw2[:], in_=dw2.rearrange("(p t) n -> p (t n)", t=4))
-        nc.sync.dma_start(out=b2bc[:], in_=db2.partition_broadcast(P))
         for c in range(2, CHUNKS):
             load_h(c)
 
@@ -214,6 +232,8 @@ def tile_vae_pb_t_kernel(tc, h_dec0, x, dw1, db1, dw2, db2, out_0, out_1):
 
         transposes(0)
         evacuate(0)
+        bias_ps = ps_a.tile([P, WIDTH], F32, name="bias_ps", tag="acc")
+        nc.tensor.matmul(out=bias_ps[:], lhsT=ones[:], rhs=brow[:], start=True, stop=True)
         transposes(1)
         evacuate(1)
         quantise0(0)
@@ -224,6 +244,7 @@ def tile_vae_pb_t_kernel(tc, h_dec0, x, dw1, db1, dw2, db2, out_0, out_1):
         )
         quantise0(1)
         nc.vector.quantize_mx(out=w2c[:].bitcast(FP8X4), scales=w2s[:], in_=wg2[:])
+        nc.vector.tensor_copy(out=b2bc[:], in_=bias_ps[:])
         layer1(0)
 
         def epilogue_step(j):
@@ -234,18 +255,23 @@ def tile_vae_pb_t_kernel(tc, h_dec0, x, dw1, db1, dw2, db2, out_0, out_1):
 
         for c in range(CHUNKS):
             silu(c)
-            if c + 2 < CHUNKS:
-                transposes(c + 2)
-                evacuate(c + 2)
+            ahead = [2, 3] if c == 0 else [c + LOOK]
+            if ahead[0] < CHUNKS:
+                transposes(ahead[0])
+                evacuate(ahead[0])
             load_x(c)
             if c + 1 < CHUNKS:
                 layer1(c + 1)
+            if c == 0:
+                transposes(ahead[1])
+                evacuate(ahead[1])
             if c >= 2:
                 for e in range(EARLY):
                     layer2(EARLY * (c - 2) + e + 2)
             regroup(c)
-            if c + 2 < CHUNKS:
-                quantise0(c + 2)
+            for n in ahead:
+                if n < CHUNKS:
+                    quantise0(n)
             quantise1(c)
             if c == 0:
                 layer2(0)
@@ -256,11 +282,11 @@ def tile_vae_pb_t_kernel(tc, h_dec0, x, dw1, db1, dw2, db2, out_0, out_1):
 
         per_group = CHUNKS // GROUPS
         finished = []
-        for e in range(EARLY):
-            layer2(EARLY * (CHUNKS - 2) + e + 2)
-        for j in range(EARLY * (CHUNKS - 1), ROWS + 1):
+        for j in range(FIRST_LATE + 2 - EARLY, FIRST_LATE + DEEP):
+            layer2(j)
+        for j in range(FIRST_LATE, ROWS + 1):
             epilogue_step(j)
-            layer2(j + 2)
+            layer2(j + DEEP)
             for c in range(len(finished), j // TILES):
                 sigmoid_store(c)
                 finished.append(c)

@@ -20,7 +20,8 @@ TILES = 4
 CHUNKS = ROWS // TILES
 CW = TILES * WIDTH
 CLAMP = -40.0
-GROUPS = 2
+GROUPS = 1
+S_FROM = 1
 EARLY = 2
 LOOK = 3
 DEEP = 8
@@ -55,6 +56,10 @@ def tile_vae_pb_t_kernel(tc, h_dec0, x, dw1, db1, dw2, db2, out_0, out_1):
         sum_lc = const.tile([P, ROWS], F32, name="sum_lc")
         sum_lx = const.tile([P, ROWS], F32, name="sum_lx")
         sum_ln = const.tile([P, ROWS], F32, name="sum_ln")
+        sum_rl = const.tile([P, ROWS], F32, name="sum_rl")
+        up = const.tile([P, 1], F32, name="up")
+        down = const.tile([P, 1], F32, name="down")
+        warm = const.tile([P, 1], F32, name="warm")
         part = const.tile([P, ROWS], F32, name="part")
         bce = const.tile([P, ROWS], F32, name="bce")
         junk = const.tile([P, WIDTH], BF16, name="junk")
@@ -76,12 +81,7 @@ def tile_vae_pb_t_kernel(tc, h_dec0, x, dw1, db1, dw2, db2, out_0, out_1):
 
         def load_h(c):
             h0[c] = io.tile([P, CW], BF16, name="h0_%d" % c, tag="io")
-            pieces = 2 if c == 0 else 1
-            step = CW // pieces
-            for i in range(pieces):
-                nc.sync.dma_start(
-                    out=h0[c][:, step * i : step * (i + 1)], in_=h_rows[:, CW * c + step * i : CW * c + step * (i + 1)]
-                )
+            nc.sync.dma_start(out=h0[c][:], in_=h_rows[:, CW * c : CW * (c + 1)])
 
         def load_x(c):
             xs[c] = io.tile([P, CW], BF16, name="x_%d" % c, tag="io")
@@ -170,8 +170,21 @@ def tile_vae_pb_t_kernel(tc, h_dec0, x, dw1, db1, dw2, db2, out_0, out_1):
             c, r = divmod(j, TILES)
             nc.vector.tensor_tensor(out=logit[c][:, r, :], in0=accs[j][:], in1=b2bc[:], op=ALU.add)
 
+        def on_scalar(j):
+            return j >= FIRST_LATE and j % TILES >= S_FROM
+
         def clamp(j):
             c, r = divmod(j, TILES)
+            if on_scalar(j):
+                nc.scalar.activation(
+                    out=recon[c][:, r, :],
+                    in_=logit[c][:, r, :],
+                    func=ACT.Relu,
+                    bias=up[:],
+                    scale=1.0,
+                    accum_out=sum_rl[:, j : j + 1],
+                )
+                return
             nc.vector.tensor_scalar(
                 out=recon[c][:, r, :],
                 in0=logit[c][:, r, :],
@@ -184,7 +197,13 @@ def tile_vae_pb_t_kernel(tc, h_dec0, x, dw1, db1, dw2, db2, out_0, out_1):
 
         def sigmoid_store(c):
             flat = recon[c][:].rearrange("p r k -> p (r k)")
-            nc.scalar.activation(out=flat, in_=flat, func=ACT.Sigmoid)
+            split = len([r for r in range(TILES) if not on_scalar(TILES * c + r)])
+            if split > 0:
+                nc.scalar.activation(out=flat[:, : WIDTH * split], in_=flat[:, : WIDTH * split], func=ACT.Sigmoid)
+            if split < TILES:
+                nc.scalar.activation(
+                    out=flat[:, WIDTH * split :], in_=flat[:, WIDTH * split :], func=ACT.Sigmoid, bias=down[:], scale=1.0
+                )
             nc.sync.dma_start(out=o_rows[:, CW * c : CW * (c + 1)], in_=flat)
 
         def log_sum(c):
@@ -206,16 +225,25 @@ def tile_vae_pb_t_kernel(tc, h_dec0, x, dw1, db1, dw2, db2, out_0, out_1):
                 )
 
         nc.scalar.dma_start(out=b1r[:], in_=db1.rearrange("(p t) -> p t", t=4))
+        nc.gpsimd.memset(warm[:], 0.0)
+        nc.scalar.activation(out=warm[:], in_=warm[:], func=ACT.Silu)
+        nc.vector.memset(up[:], -CLAMP)
+        nc.vector.memset(down[:], CLAMP)
+        nc.vector.memset(sum_rl[:], 0.0)
+        nc.vector.memset(sum_lc[:], CLAMP * WIDTH)
         nc.gpsimd.memset(brow[:], 0.0)
         nc.gpsimd.memset(ones[:], 1.0)
         make_identity(nc, ident[:])
         nc.scalar.dma_start(out=brow[0:1, :], in_=db2.rearrange("(o n) -> o n", o=1))
-        load_h(0)
+        h0[0] = io.tile([P, CW], BF16, name="h0_0", tag="io")
+        half = CW // 2
+        nc.sync.dma_start(out=h0[0][:, :half], in_=h_rows[:, :half])
         raw1 = work.tile([P, CW], BF16, name="raw1", tag="hs")
         nc.sync.dma_start(
             out=raw1[:].rearrange("p (u f) -> p u f", u=2),
             in_=dw1.rearrange("(u p e) n -> p u (e n)", u=2, p=P, e=2),
         )
+        nc.sync.dma_start(out=h0[0][:, half:], in_=h_rows[:, half:CW])
         load_h(1)
         raw2 = work.tile([P, CW], BF16, name="raw2", tag="hs")
         nc.sync.dma_start(out=raw2[:], in_=dw2.rearrange("(p t) n -> p (t n)", t=4))
@@ -295,6 +323,8 @@ def tile_vae_pb_t_kernel(tc, h_dec0, x, dw1, db1, dw2, db2, out_0, out_1):
                         log_sum(d)
         for c in range(CHUNKS):
             dot_x(c)
+            if c == 1:
+                nc.vector.tensor_tensor(out=sum_lc[:], in0=sum_lc[:], in1=sum_rl[:], op=ALU.add)
 
         nc.vector.tensor_tensor(out=part[:], in0=sum_lc[:], in1=sum_lx[:], op=ALU.subtract)
         nc.vector.tensor_tensor(out=bce[:], in0=part[:], in1=sum_ln[:], op=ALU.subtract)

@@ -21,9 +21,9 @@ CHUNKS = ROWS // TILES
 CW = TILES * WIDTH
 CLAMP = -40.0
 GROUPS = 1
-S_FROM = 1
+S_FROM = 3
 EARLY = 2
-LOOK = 3
+LOOK = 2
 DEEP = 8
 FIRST_LATE = EARLY * (CHUNKS - 1)
 
@@ -62,7 +62,7 @@ def tile_vae_pb_t_kernel(tc, h_dec0, x, dw1, db1, dw2, db2, out_0, out_1):
         warm = const.tile([P, 1], F32, name="warm")
         part = const.tile([P, ROWS], F32, name="part")
         bce = const.tile([P, ROWS], F32, name="bce")
-        junk = const.tile([P, WIDTH], BF16, name="junk")
+        junk = const.tile([P, 2 * TILES, WIDTH], BF16, name="junk")
         logit = [const.tile([P, TILES, WIDTH], F32, name="logit%d" % c) for c in range(CHUNKS)]
         recon = [const.tile([P, TILES, WIDTH], F32, name="recon%d" % c) for c in range(CHUNKS)]
         c1 = [const.tile([P, WIDTH], U32, name="c1_%d" % c, align_bytes=64) for c in range(CHUNKS)]
@@ -209,7 +209,9 @@ def tile_vae_pb_t_kernel(tc, h_dec0, x, dw1, db1, dw2, db2, out_0, out_1):
         def log_sum(c):
             for r in range(TILES):
                 j = TILES * c + r
-                nc.scalar.activation(out=junk[:], in_=recon[c][:, r, :], func=ACT.Ln, accum_out=sum_ln[:, j : j + 1])
+                nc.scalar.activation(
+                    out=junk[:, j % (2 * TILES), :], in_=recon[c][:, r, :], func=ACT.Ln, accum_out=sum_ln[:, j : j + 1]
+                )
 
         def dot_x(c):
             for r in range(TILES):
@@ -283,16 +285,13 @@ def tile_vae_pb_t_kernel(tc, h_dec0, x, dw1, db1, dw2, db2, out_0, out_1):
 
         for c in range(CHUNKS):
             silu(c)
-            ahead = [2, 3] if c == 0 else [c + LOOK]
+            ahead = [c + LOOK]
             if ahead[0] < CHUNKS:
                 transposes(ahead[0])
                 evacuate(ahead[0])
             load_x(c)
             if c + 1 < CHUNKS:
                 layer1(c + 1)
-            if c == 0:
-                transposes(ahead[1])
-                evacuate(ahead[1])
             if c >= 2:
                 for e in range(EARLY):
                     layer2(EARLY * (c - 2) + e + 2)

@@ -21,7 +21,7 @@ CHUNKS = ROWS // TILES
 CW = TILES * WIDTH
 CLAMP = -40.0
 GROUPS = 1
-S_FROM = 3
+S_FROM = 2
 EARLY = 2
 LOOK = 2
 DEEP = 8

@@ -22,7 +22,7 @@ CW = TILES * WIDTH
 CLAMP = -40.0
 GROUPS = 1
 S_FROM = 2
-EARLY = 2
+EARLY = 1
 LOOK = 2
 DEEP = 8
 FIRST_LATE = EARLY * (CHUNKS - 1)

@@ -227,16 +227,16 @@ def tile_vae_pb_t_kernel(tc, h_dec0, x, dw1, db1, dw2, db2, out_0, out_1):
                 )
 
         nc.scalar.dma_start(out=b1r[:], in_=db1.rearrange("(p t) -> p t", t=4))
+        nc.vector.memset(brow[:], 0.0)
+        nc.scalar.dma_start(out=brow[0:1, :], in_=db2.rearrange("(o n) -> o n", o=1))
         nc.gpsimd.memset(warm[:], 0.0)
         nc.scalar.activation(out=warm[:], in_=warm[:], func=ACT.Silu)
         nc.vector.memset(up[:], -CLAMP)
         nc.vector.memset(down[:], CLAMP)
         nc.vector.memset(sum_rl[:], 0.0)
         nc.vector.memset(sum_lc[:], CLAMP * WIDTH)
-        nc.gpsimd.memset(brow[:], 0.0)
-        nc.gpsimd.memset(ones[:], 1.0)
         make_identity(nc, ident[:])
-        nc.scalar.dma_start(out=brow[0:1, :], in_=db2.rearrange("(o n) -> o n", o=1))
+        nc.gpsimd.memset(ones[:], 1.0)
         h0[0] = io.tile([P, CW], BF16, name="h0_0", tag="io")
         half = CW // 2
         nc.sync.dma_start(out=h0[0][:, :half], in_=h_rows[:, :half])
@@ -262,8 +262,6 @@ def tile_vae_pb_t_kernel(tc, h_dec0, x, dw1, db1, dw2, db2, out_0, out_1):
 
         transposes(0)
         evacuate(0)
-        bias_ps = ps_a.tile([P, WIDTH], F32, name="bias_ps", tag="acc")
-        nc.tensor.matmul(out=bias_ps[:], lhsT=ones[:], rhs=brow[:], start=True, stop=True)
         transposes(1)
         evacuate(1)
         quantise0(0)
@@ -274,8 +272,10 @@ def tile_vae_pb_t_kernel(tc, h_dec0, x, dw1, db1, dw2, db2, out_0, out_1):
         )
         quantise0(1)
         nc.vector.quantize_mx(out=w2c[:].bitcast(FP8X4), scales=w2s[:], in_=wg2[:])
-        nc.vector.tensor_copy(out=b2bc[:], in_=bias_ps[:])
         layer1(0)
+        bias_ps = ps_a.tile([P, WIDTH], F32, name="bias_ps", tag="acc")
+        nc.tensor.matmul(out=bias_ps[:], lhsT=ones[:], rhs=brow[:], start=True, stop=True)
+        nc.vector.tensor_copy(out=b2bc[:], in_=bias_ps[:])
 
         def epilogue_step(j):
             if j < ROWS:
@@ -292,6 +292,9 @@ def tile_vae_pb_t_kernel(tc, h_dec0, x, dw1, db1, dw2, db2, out_0, out_1):
             load_x(c)
             if c + 1 < CHUNKS:
                 layer1(c + 1)
+            if c == 1:
+                layer2(0)
+                layer2(1)
             if c >= 2:
                 for e in range(EARLY):
                     layer2(EARLY * (c - 2) + e + 2)
@@ -300,10 +303,7 @@ def tile_vae_pb_t_kernel(tc, h_dec0, x, dw1, db1, dw2, db2, out_0, out_1):
                 if n < CHUNKS:
                     quantise0(n)
             quantise1(c)
-            if c == 0:
-                layer2(0)
-                layer2(1)
-            else:
+            if c >= 1:
                 for e in range(EARLY):
                     epilogue_step(EARLY * (c - 1) + e)
 

@@ -20,11 +20,9 @@ TILES = 4
 CHUNKS = ROWS // TILES
 CW = TILES * WIDTH
 CLAMP = -40.0
-GROUPS = 1
-S_FROM = 2
 EARLY = 1
 LOOK = 2
-DEEP = 8
+DEEP = 6
 FIRST_LATE = EARLY * (CHUNKS - 1)
 
 
@@ -53,12 +51,9 @@ def tile_vae_pb_t_kernel(tc, h_dec0, x, dw1, db1, dw2, db2, out_0, out_1):
         b2bc = const.tile([P, WIDTH], F32, name="b2bc")
         ones = const.tile([P, P], BF16, name="ones")
         brow = const.tile([P, WIDTH], BF16, name="brow")
-        sum_lc = const.tile([P, ROWS], F32, name="sum_lc")
         sum_lx = const.tile([P, ROWS], F32, name="sum_lx")
         sum_ln = const.tile([P, ROWS], F32, name="sum_ln")
-        sum_rl = const.tile([P, ROWS], F32, name="sum_rl")
-        up = const.tile([P, 1], F32, name="up")
-        down = const.tile([P, 1], F32, name="down")
+        onesf = const.tile([P, 1], F32, name="onesf")
         warm = const.tile([P, 1], F32, name="warm")
         part = const.tile([P, ROWS], F32, name="part")
         bce = const.tile([P, ROWS], F32, name="bce")
@@ -78,6 +73,8 @@ def tile_vae_pb_t_kernel(tc, h_dec0, x, dw1, db1, dw2, db2, out_0, out_1):
         hs = {}
         g1 = {}
         accs = {}
+        sums = {}
+        halves = {}
 
         def load_h(c):
             h0[c] = io.tile([P, CW], BF16, name="h0_%d" % c, tag="io")
@@ -87,9 +84,9 @@ def tile_vae_pb_t_kernel(tc, h_dec0, x, dw1, db1, dw2, db2, out_0, out_1):
             xs[c] = io.tile([P, CW], BF16, name="x_%d" % c, tag="io")
             nc.sync.dma_start(out=xs[c][:], in_=x_rows[:, CW * c : CW * (c + 1)])
 
-        def transposes(c):
+        def transposes(c, bs=(0, 1)):
             words = h0[c][:].bitcast(F32)
-            for b in range(2):
+            for b in bs:
                 xt = ps_t.tile([P, 2, 256], F32, name="xt%d_%d" % (c, b), tag="xt")
                 for r2 in range(2):
                     for u in range(2):
@@ -97,39 +94,50 @@ def tile_vae_pb_t_kernel(tc, h_dec0, x, dw1, db1, dw2, db2, out_0, out_1):
                         nc.tensor.transpose(xt[:, u, P * r2 : P * (r2 + 1)], words[:, lo : lo + P], ident[:])
                 xts[(c, b)] = xt
 
-        def evacuate(c):
-            g0[c] = work.tile([P, CW], BF16, name="g0_%d" % c, tag="g0", bufs=LOOK, align_bytes=64)
+        def evacuate(c, bs=(0, 1)):
+            if 0 in bs:
+                g0[c] = work.tile([P, CW], BF16, name="g0_%d" % c, tag="g0", bufs=LOOK, align_bytes=64)
             pairs = g0[c][:].bitcast(F32).rearrange("p (w u) -> p w u", u=2)
-            for b in range(2):
+            for b in bs:
                 nc.scalar.copy(
                     out=pairs[:, 256 * b : 256 * (b + 1), :],
                     in_=xts[(c, b)][:].rearrange("p u w -> p w u"),
                 )
 
-        def quantise0(c):
-            c0[c] = work.tile([P, WIDTH], U32, name="c0_%d" % c, tag="c0", bufs=LOOK, align_bytes=64)
-            s0[c] = work.tile([P, WIDTH], U8, name="s0_%d" % c, tag="s0", bufs=LOOK, align_bytes=64)
-            nc.vector.quantize_mx(out=c0[c][:].bitcast(FP8X4), scales=s0[c][:], in_=g0[c][:])
+        def quantise0(c, lo=0, hi=WIDTH):
+            if lo == 0:
+                c0[c] = work.tile([P, WIDTH], U32, name="c0_%d" % c, tag="c0", bufs=LOOK, align_bytes=64)
+                s0[c] = work.tile([P, WIDTH], U8, name="s0_%d" % c, tag="s0", bufs=LOOK, align_bytes=64)
+            nc.vector.quantize_mx(
+                out=c0[c][:, lo:hi].bitcast(FP8X4), scales=s0[c][:, lo:hi], in_=g0[c][:, 4 * lo : 4 * hi]
+            )
 
-        def layer1(c):
+        def layer1(c, lo=0, hi=WIDTH):
+            per_bank = WIDTH // (hi - lo)
             for t in range(4):
-                z = ps_z.tile([P, WIDTH], F32, name="z%d_%d" % (c, t), tag="z")
+                if t % per_bank == 0:
+                    z = ps_z.tile([P, per_bank, hi - lo], F32, name="z%d_%d_%d" % (c, lo, t), tag="z")
+                zs[(c, lo, t)] = z[:, t % per_bank, :]
                 nc.tensor.matmul_mx(
-                    out=z[:],
+                    out=zs[(c, lo, t)],
                     lhsT=w1c[:, P * t : P * (t + 1)].bitcast(FP8X4),
                     lhsT_scale=w1s[:, P * t : P * (t + 1)],
-                    rhs=c0[c][:].bitcast(FP8X4),
-                    rhs_scale=s0[c][:],
+                    rhs=c0[c][:, lo:hi].bitcast(FP8X4),
+                    rhs_scale=s0[c][:, lo:hi],
                     start=True,
                     stop=True,
                 )
-                zs[(c, t)] = z
 
-        def silu(c):
-            hs[c] = work.tile([P, 4, WIDTH], BF16, name="hs%d" % c, tag="hs")
-            for t in range(4):
+        def silu(c, lo=0, hi=WIDTH):
+            if lo == 0:
+                hs[c] = work.tile([P, 4, WIDTH], BF16, name="hs%d" % c, tag="hs")
+            for t in (1, 0, 3, 2):
                 nc.scalar.activation(
-                    out=hs[c][:, t, :], in_=zs[(c, t)][:], func=ACT.Silu, bias=b1f[:, t : t + 1], scale=1.0
+                    out=hs[c][:, t, lo:hi],
+                    in_=zs[(c, lo, t)],
+                    func=ACT.Silu,
+                    bias=b1f[:, t : t + 1],
+                    scale=1.0,
                 )
 
         def regroup(c):
@@ -151,10 +159,8 @@ def tile_vae_pb_t_kernel(tc, h_dec0, x, dw1, db1, dw2, db2, out_0, out_1):
             late = (j - FIRST_LATE) % DEEP if j >= FIRST_LATE else 0
             if late < 2:
                 acc = ps_a.tile([P, WIDTH], F32, name="acc%d" % j, tag="acc")
-            elif late < 6:
-                acc = ps_z.tile([P, WIDTH], F32, name="acc%d" % j, tag="z")
             else:
-                acc = ps_t.tile([P, WIDTH], F32, name="acc%d" % j, tag="xt")
+                acc = ps_z.tile([P, WIDTH], F32, name="acc%d" % j, tag="z")
             nc.tensor.matmul_mx(
                 out=acc[:],
                 lhsT=c1[c][:, P * r : P * (r + 1)].bitcast(FP8X4),
@@ -170,41 +176,57 @@ def tile_vae_pb_t_kernel(tc, h_dec0, x, dw1, db1, dw2, db2, out_0, out_1):
             c, r = divmod(j, TILES)
             nc.vector.tensor_tensor(out=logit[c][:, r, :], in0=accs[j][:], in1=b2bc[:], op=ALU.add)
 
-        def on_scalar(j):
-            return j >= FIRST_LATE and j % TILES >= S_FROM
-
         def clamp(j):
             c, r = divmod(j, TILES)
-            if on_scalar(j):
-                nc.scalar.activation(
-                    out=recon[c][:, r, :],
-                    in_=logit[c][:, r, :],
-                    func=ACT.Relu,
-                    bias=up[:],
-                    scale=1.0,
-                    accum_out=sum_rl[:, j : j + 1],
-                )
-                return
             nc.vector.tensor_scalar(
-                out=recon[c][:, r, :],
-                in0=logit[c][:, r, :],
+                out=recon[c][:, r : r + 2, :],
+                in0=logit[c][:, r : r + 2, :],
                 scalar1=CLAMP,
                 scalar2=None,
                 op0=ALU.max,
-                op1=ALU.add,
-                accum_out=sum_lc[:, j : j + 1],
             )
 
-        def sigmoid_store(c):
-            flat = recon[c][:].rearrange("p r k -> p (r k)")
-            split = len([r for r in range(TILES) if not on_scalar(TILES * c + r)])
-            if split > 0:
-                nc.scalar.activation(out=flat[:, : WIDTH * split], in_=flat[:, : WIDTH * split], func=ACT.Sigmoid)
-            if split < TILES:
-                nc.scalar.activation(
-                    out=flat[:, WIDTH * split :], in_=flat[:, WIDTH * split :], func=ACT.Sigmoid, bias=down[:], scale=1.0
+        def fold(c, rs=(0, 1, 2, 3)):
+            if 0 in rs:
+                sums[c] = ps_t.tile([P, TILES, P], F32, name="sums%d" % c, tag="xt")
+            for r in rs:
+                for b in range(4):
+                    nc.tensor.matmul(
+                        out=sums[c][:, r, :],
+                        lhsT=recon[c][:, r, P * b : P * (b + 1)],
+                        rhs=ident[:],
+                        is_transpose=True,
+                        start=b == 0,
+                        stop=b == 3,
+                    )
+
+        def unload(c, on_vector=False):
+            if c % 2 == 0:
+                if c < 4:
+                    pair = work.tile([P, 2, TILES, P], F32, name="pair%d" % c, tag="hs")
+                else:
+                    pair = work.tile([P, 2, TILES, P], F32, name="pair%d" % c, tag="g1", align_bytes=64)
+                halves[c] = pair
+                halves[c + 1] = pair
+            if on_vector:
+                nc.vector.tensor_copy(out=halves[c][:, c % 2, :, :], in_=sums[c][:])
+            else:
+                nc.scalar.copy(out=halves[c][:, c % 2, :, :], in_=sums[c][:])
+
+        def total(c):
+            for r in range(TILES):
+                nc.tensor.matmul(
+                    out=totals[:, TILES * c + r : TILES * c + r + 1],
+                    lhsT=halves[c][:, c % 2, r, :],
+                    rhs=onesf[:],
+                    start=True,
+                    stop=True,
                 )
-            nc.sync.dma_start(out=o_rows[:, CW * c : CW * (c + 1)], in_=flat)
+
+        def sigmoid_store(c, lo=0, hi=CW):
+            flat = recon[c][:].rearrange("p r k -> p (r k)")[:, lo:hi]
+            nc.scalar.activation(out=flat, in_=flat, func=ACT.Sigmoid)
+            nc.sync.dma_start(out=o_rows[:, CW * c + lo : CW * c + hi], in_=flat)
 
         def log_sum(c):
             for r in range(TILES):
@@ -231,10 +253,7 @@ def tile_vae_pb_t_kernel(tc, h_dec0, x, dw1, db1, dw2, db2, out_0, out_1):
         nc.scalar.dma_start(out=brow[0:1, :], in_=db2.rearrange("(o n) -> o n", o=1))
         nc.gpsimd.memset(warm[:], 0.0)
         nc.scalar.activation(out=warm[:], in_=warm[:], func=ACT.Silu)
-        nc.vector.memset(up[:], -CLAMP)
-        nc.vector.memset(down[:], CLAMP)
-        nc.vector.memset(sum_rl[:], 0.0)
-        nc.vector.memset(sum_lc[:], CLAMP * WIDTH)
+        nc.vector.memset(onesf[:], 1.0)
         make_identity(nc, ident[:])
         nc.gpsimd.memset(ones[:], 1.0)
         h0[0] = io.tile([P, CW], BF16, name="h0_0", tag="io")
@@ -254,17 +273,38 @@ def tile_vae_pb_t_kernel(tc, h_dec0, x, dw1, db1, dw2, db2, out_0, out_1):
 
         nc.vector.tensor_copy(out=b1f[:], in_=b1r[:])
         wg1 = work.tile([P, CW], BF16, name="wg1", tag="g1", align_bytes=64)
-        nc.vector.tensor_copy(
-            out=wg1[:].rearrange("p (s m t) -> p s m t", s=4, m=P, t=4),
-            in_=raw1[:].rearrange("p (t m s) -> p s m t", t=4, m=P, s=4),
-        )
-        nc.vector.quantize_mx(out=w1c[:].bitcast(FP8X4), scales=w1s[:], in_=wg1[:])
+        wide1 = wg1[:].rearrange("p (s m t) -> p s m t", s=4, m=P, t=4)
+        rows1 = raw1[:].rearrange("p (t m s) -> p s m t", t=4, m=P, s=4)
 
-        transposes(0)
-        evacuate(0)
+        def group1(s):
+            nc.vector.tensor_copy(out=wide1[:, s, :, :], in_=rows1[:, s, :, :])
+
+        def quant1(s):
+            cols = slice(P * s, P * (s + 1))
+            nc.vector.quantize_mx(
+                out=w1c[:, cols].bitcast(FP8X4), scales=w1s[:, cols], in_=wg1[:, 4 * P * s : 4 * P * (s + 1)]
+            )
+
+        half_w = WIDTH // 2
+        transposes(0, (0,))
+        evacuate(0, (0,))
+        group1(0)
+        group1(1)
+        quant1(0)
+        quantise0(0, 0, half_w)
+        group1(2)
+        quant1(1)
+        group1(3)
+        quant1(2)
+        quant1(3)
+        transposes(0, (1,))
+        evacuate(0, (1,))
+        layer1(0, 0, half_w)
+        silu(0, 0, half_w)
         transposes(1)
         evacuate(1)
-        quantise0(0)
+        quantise0(0, half_w, WIDTH)
+        layer1(0, half_w, WIDTH)
         wg2 = work.tile([P, CW], BF16, name="wg2", tag="g1", align_bytes=64)
         nc.vector.tensor_copy(
             out=wg2[:].rearrange("p (c i t) -> p c t i", i=4, t=4),
@@ -272,7 +312,6 @@ def tile_vae_pb_t_kernel(tc, h_dec0, x, dw1, db1, dw2, db2, out_0, out_1):
         )
         quantise0(1)
         nc.vector.quantize_mx(out=w2c[:].bitcast(FP8X4), scales=w2s[:], in_=wg2[:])
-        layer1(0)
         bias_ps = ps_a.tile([P, WIDTH], F32, name="bias_ps", tag="acc")
         nc.tensor.matmul(out=bias_ps[:], lhsT=ones[:], rhs=brow[:], start=True, stop=True)
         nc.vector.tensor_copy(out=b2bc[:], in_=bias_ps[:])
@@ -280,11 +319,14 @@ def tile_vae_pb_t_kernel(tc, h_dec0, x, dw1, db1, dw2, db2, out_0, out_1):
         def epilogue_step(j):
             if j < ROWS:
                 add_bias(j)
-            if j >= 1:
-                clamp(j - 1)
+            if j >= 3 and j % 2 == 1:
+                clamp(j - 3)
 
         for c in range(CHUNKS):
-            silu(c)
+            if c == 0:
+                silu(0, half_w, WIDTH)
+            else:
+                silu(c)
             ahead = [c + LOOK]
             if ahead[0] < CHUNKS:
                 transposes(ahead[0])
@@ -292,6 +334,8 @@ def tile_vae_pb_t_kernel(tc, h_dec0, x, dw1, db1, dw2, db2, out_0, out_1):
             load_x(c)
             if c + 1 < CHUNKS:
                 layer1(c + 1)
+            if c == CHUNKS - 1:
+                fold(0)
             if c == 1:
                 layer2(0)
                 layer2(1)
@@ -307,24 +351,35 @@ def tile_vae_pb_t_kernel(tc, h_dec0, x, dw1, db1, dw2, db2, out_0, out_1):
                 for e in range(EARLY):
                     epilogue_step(EARLY * (c - 1) + e)
 
-        per_group = CHUNKS // GROUPS
-        finished = []
         for j in range(FIRST_LATE + 2 - EARLY, FIRST_LATE + DEEP):
             layer2(j)
-        for j in range(FIRST_LATE, ROWS + 1):
+        sigmoid_store(0)
+        unload(0)
+        for j in range(FIRST_LATE, ROWS):
             epilogue_step(j)
             layer2(j + DEEP)
-            for c in range(len(finished), j // TILES):
-                sigmoid_store(c)
-                finished.append(c)
-                if len(finished) % per_group == 0:
-                    for d in finished[-per_group:]:
-                        log_sum(d)
+            if j % 2 == 1:
+                c, r = divmod(j - 3, TILES)
+                if c > 0:
+                    fold(c, (r, r + 1))
+                    if r == 2:
+                        sigmoid_store(c)
+                        if c < CHUNKS - 2:
+                            unload(c)
+        c = CHUNKS - 1
+        sigmoid_store(c, 0, CW // 2)
+        clamp(ROWS - 2)
+        fold(c, (2, 3))
+        sigmoid_store(c, CW // 2, CW)
+        unload(c - 1, True)
+        unload(c, True)
+        totals = ps_a.tile([P, ROWS], F32, name="totals", tag="acc")
+        for c in range(CHUNKS):
+            total(c)
+            log_sum(c)
         for c in range(CHUNKS):
             dot_x(c)
-            if c == 1:
-                nc.vector.tensor_tensor(out=sum_lc[:], in0=sum_lc[:], in1=sum_rl[:], op=ALU.add)
 
-        nc.vector.tensor_tensor(out=part[:], in0=sum_lc[:], in1=sum_lx[:], op=ALU.subtract)
+        nc.vector.tensor_tensor(out=part[:], in0=totals[:], in1=sum_lx[:], op=ALU.subtract)
         nc.vector.tensor_tensor(out=bce[:], in0=part[:], in1=sum_ln[:], op=ALU.subtract)
         nc.sync.dma_start(out=out_0.rearrange("(p q) -> p q", q=ROWS), in_=bce[:])

@@ -21,9 +21,18 @@ CHUNKS = ROWS // TILES
 CW = TILES * WIDTH
 CLAMP = -40.0
 EARLY = 1
+GCOLS = (0, 256, 256, 256, 256, 256, 256, 256)
+ADDS = (0, 2, 3, 3, 3, 3, 3, 3)
+CL = (0, 0, 0, 0, 1, 1, 0, 0)
+UV = (4, 5, 6, 7)
+FOLDS = (0, 0, 0, 0, 0, 0, 1, 1)
+AHEAD = 2
+DOTS = 0
+DFROM = 3
 LOOK = 2
 DEEP = 6
-FIRST_LATE = EARLY * (CHUNKS - 1)
+PAIRS = ()
+FIRST_LATE = sum(ADDS)
 
 
 def tile_vae_pb_t_kernel(tc, h_dec0, x, dw1, db1, dw2, db2, out_0, out_1):
@@ -75,6 +84,7 @@ def tile_vae_pb_t_kernel(tc, h_dec0, x, dw1, db1, dw2, db2, out_0, out_1):
         accs = {}
         sums = {}
         halves = {}
+        twos = {}
 
         def load_h(c):
             h0[c] = io.tile([P, CW], BF16, name="h0_%d" % c, tag="io")
@@ -142,10 +152,21 @@ def tile_vae_pb_t_kernel(tc, h_dec0, x, dw1, db1, dw2, db2, out_0, out_1):
 
         def regroup(c):
             g1[c] = work.tile([P, WIDTH, 4], BF16, name="g1_%d" % c, tag="g1", align_bytes=64)
-            nc.vector.tensor_copy(
-                out=g1[c][:].rearrange("p (c i) t -> p c t i", i=4),
-                in_=hs[c][:].rearrange("p t (c i) -> p c t i", i=4),
-            )
+            cut = WIDTH - GCOLS[c]
+            if cut > 0:
+                nc.vector.tensor_copy(
+                    out=g1[c][:, :cut, :].rearrange("p (c i) t -> p c t i", i=4),
+                    in_=hs[c][:, :, :cut].rearrange("p t (c i) -> p c t i", i=4),
+                )
+            if cut < WIDTH:
+                nc.gpsimd.tensor_scalar(
+                    out=g1[c][:, cut:, :],
+                    in0=hs[c][:, :, cut:].rearrange("p t n -> p n t"),
+                    scalar1=1.0,
+                    scalar2=0.0,
+                    op0=ALU.mult,
+                    op1=ALU.add,
+                )
 
         def quantise1(c):
             nc.vector.quantize_mx(
@@ -176,11 +197,10 @@ def tile_vae_pb_t_kernel(tc, h_dec0, x, dw1, db1, dw2, db2, out_0, out_1):
             c, r = divmod(j, TILES)
             nc.vector.tensor_tensor(out=logit[c][:, r, :], in0=accs[j][:], in1=b2bc[:], op=ALU.add)
 
-        def clamp(j):
-            c, r = divmod(j, TILES)
+        def clamp(c, lo=0, hi=TILES):
             nc.vector.tensor_scalar(
-                out=recon[c][:, r : r + 2, :],
-                in0=logit[c][:, r : r + 2, :],
+                out=recon[c][:, lo:hi, :],
+                in0=logit[c][:, lo:hi, :],
                 scalar1=CLAMP,
                 scalar2=None,
                 op0=ALU.max,
@@ -228,16 +248,33 @@ def tile_vae_pb_t_kernel(tc, h_dec0, x, dw1, db1, dw2, db2, out_0, out_1):
             nc.scalar.activation(out=flat, in_=flat, func=ACT.Sigmoid)
             nc.sync.dma_start(out=o_rows[:, CW * c + lo : CW * c + hi], in_=flat)
 
+        def pair(c):
+            flat = recon[c][:].rearrange("p r k -> p (r k)")
+            for r in range(TILES):
+                if TILES * c + r in PAIRS:
+                    twos[TILES * c + r] = work.tile([P, WIDTH // 2], F32, name="two%d_%d" % (c, r), tag="c0", bufs=LOOK, align_bytes=64)
+                    nc.vector.tensor_tensor(
+                        out=twos[TILES * c + r][:],
+                        in0=recon[c][:, r, : WIDTH // 2],
+                        in1=recon[c][:, r, WIDTH // 2 :],
+                        op=ALU.mult,
+                    )
+
         def log_sum(c):
             for r in range(TILES):
                 j = TILES * c + r
+                if j in PAIRS:
+                    nc.scalar.activation(
+                        out=junk[:, j % (2 * TILES), : WIDTH // 2], in_=twos[j][:], func=ACT.Ln, accum_out=sum_ln[:, j : j + 1]
+                    )
+                    continue
                 nc.scalar.activation(
                     out=junk[:, j % (2 * TILES), :], in_=recon[c][:, r, :], func=ACT.Ln, accum_out=sum_ln[:, j : j + 1]
                 )
 
-        def dot_x(c):
-            for r in range(TILES):
-                j = TILES * c + r
+        def dot_x(n):
+            for j in range(state["dots"], min(ROWS, state["dots"] + n)):
+                c, r = divmod(j, TILES)
                 nc.vector.scalar_tensor_tensor(
                     out=logit[c][:, r, :],
                     in0=logit[c][:, r, :],
@@ -247,6 +284,7 @@ def tile_vae_pb_t_kernel(tc, h_dec0, x, dw1, db1, dw2, db2, out_0, out_1):
                     op1=ALU.mult,
                     accum_out=sum_lx[:, j : j + 1],
                 )
+            state["dots"] = min(ROWS, state["dots"] + n)
 
         nc.scalar.dma_start(out=b1r[:], in_=db1.rearrange("(p t) -> p t", t=4))
         nc.vector.memset(brow[:], 0.0)
@@ -288,6 +326,9 @@ def tile_vae_pb_t_kernel(tc, h_dec0, x, dw1, db1, dw2, db2, out_0, out_1):
         half_w = WIDTH // 2
         transposes(0, (0,))
         evacuate(0, (0,))
+        bias_ps = ps_a.tile([P, WIDTH], F32, name="bias_ps", tag="acc")
+        nc.tensor.matmul(out=bias_ps[:], lhsT=ones[:], rhs=brow[:], start=True, stop=True)
+        nc.scalar.copy(out=b2bc[:], in_=bias_ps[:])
         group1(0)
         group1(1)
         quant1(0)
@@ -312,73 +353,76 @@ def tile_vae_pb_t_kernel(tc, h_dec0, x, dw1, db1, dw2, db2, out_0, out_1):
         )
         quantise0(1)
         nc.vector.quantize_mx(out=w2c[:].bitcast(FP8X4), scales=w2s[:], in_=wg2[:])
-        bias_ps = ps_a.tile([P, WIDTH], F32, name="bias_ps", tag="acc")
-        nc.tensor.matmul(out=bias_ps[:], lhsT=ones[:], rhs=brow[:], start=True, stop=True)
-        nc.vector.tensor_copy(out=b2bc[:], in_=bias_ps[:])
 
-        def epilogue_step(j):
-            if j < ROWS:
-                add_bias(j)
-            if j >= 3 and j % 2 == 1:
-                clamp(j - 3)
+        state = {"added": 0, "issued": 0, "clamped": 0, "dots": 0}
+
+        def issue(n):
+            for k in range(n):
+                if state["issued"] < ROWS:
+                    layer2(state["issued"])
+                    state["issued"] += 1
+
+        def add_some(n, depth, stop):
+            for k in range(n):
+                add_bias(state["added"])
+                state["added"] += 1
+                if state["issued"] - state["added"] < depth and state["issued"] < stop:
+                    issue(1)
 
         for c in range(CHUNKS):
             if c == 0:
                 silu(0, half_w, WIDTH)
             else:
                 silu(c)
-            ahead = [c + LOOK]
-            if ahead[0] < CHUNKS:
-                transposes(ahead[0])
-                evacuate(ahead[0])
+            if c + LOOK < CHUNKS:
+                transposes(c + LOOK)
+                evacuate(c + LOOK)
             load_x(c)
             if c + 1 < CHUNKS:
                 layer1(c + 1)
-            if c == CHUNKS - 1:
-                fold(0)
-            if c == 1:
-                layer2(0)
-                layer2(1)
-            if c >= 2:
-                for e in range(EARLY):
-                    layer2(EARLY * (c - 2) + e + 2)
+            for k in range(FOLDS[c]):
+                fold(len(sums))
+            n = min(ADDS[c], TILES * c - state["added"])
+            stop = TILES * c
+            issue(min(stop - state["issued"], 2 - (state["issued"] - state["added"])))
             regroup(c)
-            for n in ahead:
-                if n < CHUNKS:
-                    quantise0(n)
+            add_some(n, 2, stop)
+            if c + LOOK < CHUNKS:
+                quantise0(c + LOOK)
             quantise1(c)
-            if c >= 1:
-                for e in range(EARLY):
-                    epilogue_step(EARLY * (c - 1) + e)
+            for k in range(CL[c]):
+                clamp(state["clamped"])
+                state["clamped"] += 1
 
-        for j in range(FIRST_LATE + 2 - EARLY, FIRST_LATE + DEEP):
-            layer2(j)
-        sigmoid_store(0)
-        unload(0)
-        for j in range(FIRST_LATE, ROWS):
-            epilogue_step(j)
-            layer2(j + DEEP)
-            if j % 2 == 1:
-                c, r = divmod(j - 3, TILES)
-                if c > 0:
-                    fold(c, (r, r + 1))
-                    if r == 2:
-                        sigmoid_store(c)
-                        if c < CHUNKS - 2:
-                            unload(c)
-        c = CHUNKS - 1
-        sigmoid_store(c, 0, CW // 2)
-        clamp(ROWS - 2)
-        fold(c, (2, 3))
-        sigmoid_store(c, CW // 2, CW)
-        unload(c - 1, True)
-        unload(c, True)
+        issue(DEEP - (state["issued"] - state["added"]))
+        for c in range(CHUNKS):
+            if c >= state["clamped"]:
+                add_some(min(ROWS, TILES * (c + 1) + AHEAD) - state["added"], DEEP, ROWS)
+                if c == CHUNKS - 1:
+                    for lo in (0, 2):
+                        clamp(c, lo, lo + 2)
+                        fold(c, (lo, lo + 1))
+                        sigmoid_store(c, WIDTH * lo, WIDTH * (lo + 2))
+                else:
+                    clamp(c)
+                state["clamped"] += 1
+            if c < CHUNKS - 1:
+                if c not in sums:
+                    fold(c)
+                sigmoid_store(c)
+            if c not in UV:
+                unload(c)
+            if c >= DFROM:
+                dot_x(DOTS)
+        for c in UV:
+            unload(c, True)
         totals = ps_a.tile([P, ROWS], F32, name="totals", tag="acc")
         for c in range(CHUNKS):
             total(c)
-            log_sum(c)
         for c in range(CHUNKS):
-            dot_x(c)
+            dot_x(TILES * (c + 1) - state["dots"] if TILES * (c + 1) > state["dots"] else 0)
+            pair(c)
+            log_sum(c)
 
         nc.vector.tensor_tensor(out=part[:], in0=totals[:], in1=sum_lx[:], op=ALU.subtract)
         nc.vector.tensor_tensor(out=bce[:], in0=part[:], in1=sum_ln[:], op=ALU.subtract)

@@ -20,17 +20,20 @@ TILES = 4
 CHUNKS = ROWS // TILES
 CW = TILES * WIDTH
 CLAMP = -40.0
-EARLY = 1
-GCOLS = (0, 256, 256, 256, 256, 256, 256, 256)
-ADDS = (0, 2, 3, 3, 3, 3, 3, 3)
+BIAS_S = False
+VLAG = 2
+TPOS = 1
+LAP = 8
+GCOLS = (0, 0, 288, 288, 288, 288, 288, 288)
+ADDS = (0, 0, 3, 3, 3, 3, 3, 3)
 CL = (0, 0, 0, 0, 1, 1, 0, 0)
-UV = (4, 5, 6, 7)
+UV = (5, 6, 7)
 FOLDS = (0, 0, 0, 0, 0, 0, 1, 1)
-AHEAD = 2
+AHEAD = 1
 DOTS = 0
 DFROM = 3
 LOOK = 2
-DEEP = 6
+DEEP = 4
 PAIRS = ()
 FIRST_LATE = sum(ADDS)
 
@@ -46,7 +49,8 @@ def tile_vae_pb_t_kernel(tc, h_dec0, x, dw1, db1, dw2, db2, out_0, out_1):
         io = ctx.enter_context(tc.tile_pool(name="io", bufs=CHUNKS))
         work = ctx.enter_context(tc.tile_pool(name="work", bufs=2))
         ps_t = ctx.enter_context(tc.psum_pool(name="ps_t", bufs=2))
-        ps_z = ctx.enter_context(tc.psum_pool(name="ps_z", bufs=4))
+        ps_y = ctx.enter_context(tc.psum_pool(name="ps_y", bufs=2))
+        ps_z = ctx.enter_context(tc.psum_pool(name="ps_z", bufs=2))
         ps_a = ctx.enter_context(tc.psum_pool(name="ps_a", bufs=2))
         ctx.enter_context(tc.manual_schedule())
 
@@ -126,7 +130,8 @@ def tile_vae_pb_t_kernel(tc, h_dec0, x, dw1, db1, dw2, db2, out_0, out_1):
             per_bank = WIDTH // (hi - lo)
             for t in range(4):
                 if t % per_bank == 0:
-                    z = ps_z.tile([P, per_bank, hi - lo], F32, name="z%d_%d_%d" % (c, lo, t), tag="z")
+                    pool, tag = (ps_y, "y") if t < 2 else (ps_z, "z")
+                    z = pool.tile([P, per_bank, hi - lo], F32, name="z%d_%d_%d" % (c, lo, t), tag=tag)
                 zs[(c, lo, t)] = z[:, t % per_bank, :]
                 nc.tensor.matmul_mx(
                     out=zs[(c, lo, t)],
@@ -153,10 +158,11 @@ def tile_vae_pb_t_kernel(tc, h_dec0, x, dw1, db1, dw2, db2, out_0, out_1):
         def regroup(c):
             g1[c] = work.tile([P, WIDTH, 4], BF16, name="g1_%d" % c, tag="g1", align_bytes=64)
             cut = WIDTH - GCOLS[c]
+            own = min(WIDTH, cut + LAP)
             if cut > 0:
                 nc.vector.tensor_copy(
-                    out=g1[c][:, :cut, :].rearrange("p (c i) t -> p c t i", i=4),
-                    in_=hs[c][:, :, :cut].rearrange("p t (c i) -> p c t i", i=4),
+                    out=g1[c][:, :own, :].rearrange("p (c i) t -> p c t i", i=4),
+                    in_=hs[c][:, :, :own].rearrange("p t (c i) -> p c t i", i=4),
                 )
             if cut < WIDTH:
                 nc.gpsimd.tensor_scalar(
@@ -177,11 +183,10 @@ def tile_vae_pb_t_kernel(tc, h_dec0, x, dw1, db1, dw2, db2, out_0, out_1):
             if j >= ROWS:
                 return
             c, r = divmod(j, TILES)
-            late = (j - FIRST_LATE) % DEEP if j >= FIRST_LATE else 0
-            if late < 2:
-                acc = ps_a.tile([P, WIDTH], F32, name="acc%d" % j, tag="acc")
+            if j >= FIRST_LATE + 2 and j // 2 % 2 == 0:
+                acc = ps_y.tile([P, WIDTH], F32, name="acc%d" % j, tag="y")
             else:
-                acc = ps_z.tile([P, WIDTH], F32, name="acc%d" % j, tag="z")
+                acc = ps_a.tile([P, WIDTH], F32, name="acc%d" % j, tag="acc")
             nc.tensor.matmul_mx(
                 out=acc[:],
                 lhsT=c1[c][:, P * r : P * (r + 1)].bitcast(FP8X4),
@@ -208,7 +213,8 @@ def tile_vae_pb_t_kernel(tc, h_dec0, x, dw1, db1, dw2, db2, out_0, out_1):
 
         def fold(c, rs=(0, 1, 2, 3)):
             if 0 in rs:
-                sums[c] = ps_t.tile([P, TILES, P], F32, name="sums%d" % c, tag="xt")
+                pool, tag = (ps_t, "xt") if c // 2 % 2 == 0 else (ps_z, "z")
+                sums[c] = pool.tile([P, TILES, P], F32, name="sums%d" % c, tag=tag)
             for r in rs:
                 for b in range(4):
                     nc.tensor.matmul(
@@ -326,9 +332,6 @@ def tile_vae_pb_t_kernel(tc, h_dec0, x, dw1, db1, dw2, db2, out_0, out_1):
         half_w = WIDTH // 2
         transposes(0, (0,))
         evacuate(0, (0,))
-        bias_ps = ps_a.tile([P, WIDTH], F32, name="bias_ps", tag="acc")
-        nc.tensor.matmul(out=bias_ps[:], lhsT=ones[:], rhs=brow[:], start=True, stop=True)
-        nc.scalar.copy(out=b2bc[:], in_=bias_ps[:])
         group1(0)
         group1(1)
         quant1(0)
@@ -354,6 +357,7 @@ def tile_vae_pb_t_kernel(tc, h_dec0, x, dw1, db1, dw2, db2, out_0, out_1):
         quantise0(1)
         nc.vector.quantize_mx(out=w2c[:].bitcast(FP8X4), scales=w2s[:], in_=wg2[:])
 
+        transposes(LOOK)
         state = {"added": 0, "issued": 0, "clamped": 0, "dots": 0}
 
         def issue(n):
@@ -375,26 +379,44 @@ def tile_vae_pb_t_kernel(tc, h_dec0, x, dw1, db1, dw2, db2, out_0, out_1):
             else:
                 silu(c)
             if c + LOOK < CHUNKS:
-                transposes(c + LOOK)
                 evacuate(c + LOOK)
             load_x(c)
             if c + 1 < CHUNKS:
                 layer1(c + 1)
+            if c + LOOK + 1 < CHUNKS and TPOS == 0:
+                transposes(c + LOOK + 1)
             for k in range(FOLDS[c]):
                 fold(len(sums))
+            if c == 0:
+                bias_ps = ps_a.tile([P, WIDTH], F32, name="bias_ps", tag="acc")
+                nc.tensor.matmul(out=bias_ps[:], lhsT=ones[:], rhs=brow[:], start=True, stop=True)
             n = min(ADDS[c], TILES * c - state["added"])
             stop = TILES * c
             issue(min(stop - state["issued"], 2 - (state["issued"] - state["added"])))
             regroup(c)
             add_some(n, 2, stop)
+            if c + LOOK + 1 < CHUNKS and TPOS == 1:
+                transposes(c + LOOK + 1)
             if c + LOOK < CHUNKS:
                 quantise0(c + LOOK)
             quantise1(c)
+            if c == 0:
+                if BIAS_S:
+                    nc.scalar.copy(out=b2bc[:], in_=bias_ps[:])
+                else:
+                    nc.vector.tensor_copy(out=b2bc[:], in_=bias_ps[:])
             for k in range(CL[c]):
                 clamp(state["clamped"])
                 state["clamped"] += 1
 
         issue(DEEP - (state["issued"] - state["added"]))
+
+        def unload_v(c):
+            if c in UV and c in sums and c not in halves_done:
+                unload(c, True)
+                halves_done.add(c)
+
+        halves_done = set()
         for c in range(CHUNKS):
             if c >= state["clamped"]:
                 add_some(min(ROWS, TILES * (c + 1) + AHEAD) - state["added"], DEEP, ROWS)
@@ -406,6 +428,8 @@ def tile_vae_pb_t_kernel(tc, h_dec0, x, dw1, db1, dw2, db2, out_0, out_1):
                 else:
                     clamp(c)
                 state["clamped"] += 1
+            if c >= VLAG:
+                unload_v(c - VLAG)
             if c < CHUNKS - 1:
                 if c not in sums:
                     fold(c)
@@ -414,8 +438,8 @@ def tile_vae_pb_t_kernel(tc, h_dec0, x, dw1, db1, dw2, db2, out_0, out_1):
                 unload(c)
             if c >= DFROM:
                 dot_x(DOTS)
-        for c in UV:
-            unload(c, True)
+        for c in range(CHUNKS):
+            unload_v(c)
         totals = ps_a.tile([P, ROWS], F32, name="totals", tag="acc")
         for c in range(CHUNKS):
             total(c)

@@ -22,9 +22,10 @@ CW = TILES * WIDTH
 CLAMP = -40.0
 BIAS_S = False
 VLAG = 2
+ULAG = 1
 TPOS = 1
 LAP = 8
-GCOLS = (0, 0, 288, 288, 288, 288, 288, 288)
+GCOLS = (0, 0, 192, 192, 192, 192, 192, 192)
 ADDS = (0, 0, 3, 3, 3, 3, 3, 3)
 CL = (0, 0, 0, 0, 1, 1, 0, 0)
 UV = (5, 6, 7)
@@ -34,7 +35,9 @@ DOTS = 0
 DFROM = 3
 LOOK = 2
 DEEP = 4
-PAIRS = ()
+NPAIR = (0, 0, 0, 0, 0, 0, 0, 0)
+PRODUCTS = ()
+WARM = (0,)
 FIRST_LATE = sum(ADDS)
 
 
@@ -88,7 +91,6 @@ def tile_vae_pb_t_kernel(tc, h_dec0, x, dw1, db1, dw2, db2, out_0, out_1):
         accs = {}
         sums = {}
         halves = {}
-        twos = {}
 
         def load_h(c):
             h0[c] = io.tile([P, CW], BF16, name="h0_%d" % c, tag="io")
@@ -200,15 +202,18 @@ def tile_vae_pb_t_kernel(tc, h_dec0, x, dw1, db1, dw2, db2, out_0, out_1):
 
         def add_bias(j):
             c, r = divmod(j, TILES)
-            nc.vector.tensor_tensor(out=logit[c][:, r, :], in0=accs[j][:], in1=b2bc[:], op=ALU.add)
+            nc.vector.scalar_tensor_tensor(
+                out=logit[c][:, r, :], in0=accs[j][:], scalar=-1.0, in1=b2bc[:], op0=ALU.mult, op1=ALU.subtract
+            )
 
         def clamp(c, lo=0, hi=TILES):
             nc.vector.tensor_scalar(
                 out=recon[c][:, lo:hi, :],
                 in0=logit[c][:, lo:hi, :],
-                scalar1=CLAMP,
-                scalar2=None,
-                op0=ALU.max,
+                scalar1=-CLAMP,
+                scalar2=-1.0,
+                op0=ALU.min,
+                op1=ALU.mult,
             )
 
         def fold(c, rs=(0, 1, 2, 3)):
@@ -216,6 +221,10 @@ def tile_vae_pb_t_kernel(tc, h_dec0, x, dw1, db1, dw2, db2, out_0, out_1):
                 pool, tag = (ps_t, "xt") if c // 2 % 2 == 0 else (ps_z, "z")
                 sums[c] = pool.tile([P, TILES, P], F32, name="sums%d" % c, tag=tag)
             for r in rs:
+                if r in WARM:
+                    free = sums[c][:, r:, :].rearrange("p r n -> p (r n)")
+                    nc.tensor.matmul(out=free, lhsT=ones[:], rhs=brow[:, : P * (TILES - r)], start=True, stop=True)
+                last = not on_gpsimd(TILES * c + r)
                 for b in range(4):
                     nc.tensor.matmul(
                         out=sums[c][:, r, :],
@@ -223,8 +232,32 @@ def tile_vae_pb_t_kernel(tc, h_dec0, x, dw1, db1, dw2, db2, out_0, out_1):
                         rhs=ident[:],
                         is_transpose=True,
                         start=b == 0,
-                        stop=b == 3,
+                        stop=last and b == 3,
                     )
+
+        def on_gpsimd(j):
+            return j in PRODUCTS
+
+        def product(j):
+            c, r = divmod(j, TILES)
+            nc.gpsimd.tensor_tensor(
+                out=logit[c][:, r, :],
+                in0=logit[c][:, r, :],
+                in1=xs[c][:, WIDTH * r : WIDTH * (r + 1)],
+                op=ALU.mult,
+            )
+
+        def fold_product(j):
+            c, r = divmod(j, TILES)
+            for b in range(4):
+                nc.tensor.matmul(
+                    out=sums[c][:, r, :],
+                    lhsT=logit[c][:, r, P * b : P * (b + 1)],
+                    rhs=ident[:],
+                    is_transpose=True,
+                    start=False,
+                    stop=b == 3,
+                )
 
         def unload(c, on_vector=False):
             if c % 2 == 0:
@@ -255,23 +288,24 @@ def tile_vae_pb_t_kernel(tc, h_dec0, x, dw1, db1, dw2, db2, out_0, out_1):
             nc.sync.dma_start(out=o_rows[:, CW * c + lo : CW * c + hi], in_=flat)
 
         def pair(c):
-            flat = recon[c][:].rearrange("p r k -> p (r k)")
-            for r in range(TILES):
-                if TILES * c + r in PAIRS:
-                    twos[TILES * c + r] = work.tile([P, WIDTH // 2], F32, name="two%d_%d" % (c, r), tag="c0", bufs=LOOK, align_bytes=64)
-                    nc.vector.tensor_tensor(
-                        out=twos[TILES * c + r][:],
-                        in0=recon[c][:, r, : WIDTH // 2],
-                        in1=recon[c][:, r, WIDTH // 2 :],
-                        op=ALU.mult,
-                    )
+            n = NPAIR[c]
+            if n > 0:
+                nc.vector.tensor_tensor(
+                    out=logit[c][:, TILES - n :, : WIDTH // 2],
+                    in0=recon[c][:, TILES - n :, : WIDTH // 2],
+                    in1=recon[c][:, TILES - n :, WIDTH // 2 :],
+                    op=ALU.mult,
+                )
 
         def log_sum(c):
             for r in range(TILES):
                 j = TILES * c + r
-                if j in PAIRS:
+                if r >= TILES - NPAIR[c]:
                     nc.scalar.activation(
-                        out=junk[:, j % (2 * TILES), : WIDTH // 2], in_=twos[j][:], func=ACT.Ln, accum_out=sum_ln[:, j : j + 1]
+                        out=junk[:, j % (2 * TILES), : WIDTH // 2],
+                        in_=logit[c][:, r, : WIDTH // 2],
+                        func=ACT.Ln,
+                        accum_out=sum_ln[:, j : j + 1],
                     )
                     continue
                 nc.scalar.activation(
@@ -281,6 +315,8 @@ def tile_vae_pb_t_kernel(tc, h_dec0, x, dw1, db1, dw2, db2, out_0, out_1):
         def dot_x(n):
             for j in range(state["dots"], min(ROWS, state["dots"] + n)):
                 c, r = divmod(j, TILES)
+                if on_gpsimd(j):
+                    continue
                 nc.vector.scalar_tensor_tensor(
                     out=logit[c][:, r, :],
                     in0=logit[c][:, r, :],
@@ -298,6 +334,7 @@ def tile_vae_pb_t_kernel(tc, h_dec0, x, dw1, db1, dw2, db2, out_0, out_1):
         nc.gpsimd.memset(warm[:], 0.0)
         nc.scalar.activation(out=warm[:], in_=warm[:], func=ACT.Silu)
         nc.vector.memset(onesf[:], 1.0)
+        nc.vector.memset(sum_lx[:], 0.0)
         make_identity(nc, ident[:])
         nc.gpsimd.memset(ones[:], 1.0)
         h0[0] = io.tile([P, CW], BF16, name="h0_0", tag="io")
@@ -418,28 +455,36 @@ def tile_vae_pb_t_kernel(tc, h_dec0, x, dw1, db1, dw2, db2, out_0, out_1):
 
         halves_done = set()
         for c in range(CHUNKS):
+            before = [j for j in range(TILES * (c - 1), TILES * c) if j in PRODUCTS]
+            for j in before:
+                product(j)
             if c >= state["clamped"]:
                 add_some(min(ROWS, TILES * (c + 1) + AHEAD) - state["added"], DEEP, ROWS)
-                if c == CHUNKS - 1:
-                    for lo in (0, 2):
-                        clamp(c, lo, lo + 2)
-                        fold(c, (lo, lo + 1))
-                        sigmoid_store(c, WIDTH * lo, WIDTH * (lo + 2))
-                else:
+                if c < CHUNKS - 1:
                     clamp(c)
                 state["clamped"] += 1
+            for j in before:
+                fold_product(j)
+            if c == CHUNKS - 1:
+                for lo in (0, 2):
+                    clamp(c, lo, lo + 2)
+                    fold(c, (lo, lo + 1))
+                    sigmoid_store(c, WIDTH * lo, WIDTH * (lo + 2))
             if c >= VLAG:
                 unload_v(c - VLAG)
             if c < CHUNKS - 1:
                 if c not in sums:
                     fold(c)
                 sigmoid_store(c)
-            if c not in UV:
-                unload(c)
+            if c >= ULAG and c - ULAG not in UV:
+                unload(c - ULAG)
             if c >= DFROM:
                 dot_x(DOTS)
         for c in range(CHUNKS):
             unload_v(c)
+        for c in range(CHUNKS - ULAG, CHUNKS):
+            if c not in UV:
+                unload(c)
         totals = ps_a.tile([P, ROWS], F32, name="totals", tag="acc")
         for c in range(CHUNKS):
             total(c)
@@ -448,6 +493,6 @@ def tile_vae_pb_t_kernel(tc, h_dec0, x, dw1, db1, dw2, db2, out_0, out_1):
             pair(c)
             log_sum(c)
 
-        nc.vector.tensor_tensor(out=part[:], in0=totals[:], in1=sum_lx[:], op=ALU.subtract)
+        nc.vector.tensor_tensor(out=part[:], in0=totals[:], in1=sum_lx[:], op=ALU.add)
         nc.vector.tensor_tensor(out=bce[:], in0=part[:], in1=sum_ln[:], op=ALU.subtract)
         nc.sync.dma_start(out=out_0.rearrange("(p q) -> p q", q=ROWS), in_=bce[:])

@@ -21,22 +21,21 @@ CHUNKS = ROWS // TILES
 CW = TILES * WIDTH
 CLAMP = -40.0
 BIAS_S = False
-VLAG = 2
-ULAG = 1
+VLAG = 8
 TPOS = 1
 LAP = 8
-GCOLS = (0, 0, 192, 192, 192, 192, 192, 192)
+GCOLS = (0, 0, 288, 288, 288, 288, 288, 288)
 ADDS = (0, 0, 3, 3, 3, 3, 3, 3)
 CL = (0, 0, 0, 0, 1, 1, 0, 0)
-UV = (5, 6, 7)
+UV = (4, 5, 6, 7)
 FOLDS = (0, 0, 0, 0, 0, 0, 1, 1)
 AHEAD = 1
 DOTS = 0
 DFROM = 3
 LOOK = 2
 DEEP = 4
-NPAIR = (0, 0, 0, 0, 0, 0, 0, 0)
-PRODUCTS = ()
+NPAIR = (0, 0, 0, 0, 0, 0, 4, 4)
+SLO = 2
 WARM = (0,)
 FIRST_LATE = sum(ADDS)
 
@@ -70,6 +69,9 @@ def tile_vae_pb_t_kernel(tc, h_dec0, x, dw1, db1, dw2, db2, out_0, out_1):
         sum_lx = const.tile([P, ROWS], F32, name="sum_lx")
         sum_ln = const.tile([P, ROWS], F32, name="sum_ln")
         onesf = const.tile([P, 1], F32, name="onesf")
+        up = const.tile([P, 1], F32, name="up")
+        down = const.tile([P, 1], F32, name="down")
+        sum_rl = const.tile([P, CHUNKS], F32, name="sum_rl")
         warm = const.tile([P, 1], F32, name="warm")
         part = const.tile([P, ROWS], F32, name="part")
         bce = const.tile([P, ROWS], F32, name="bce")
@@ -202,18 +204,30 @@ def tile_vae_pb_t_kernel(tc, h_dec0, x, dw1, db1, dw2, db2, out_0, out_1):
 
         def add_bias(j):
             c, r = divmod(j, TILES)
-            nc.vector.scalar_tensor_tensor(
-                out=logit[c][:, r, :], in0=accs[j][:], scalar=-1.0, in1=b2bc[:], op0=ALU.mult, op1=ALU.subtract
-            )
+            nc.vector.tensor_tensor(out=logit[c][:, r, :], in0=accs[j][:], in1=b2bc[:], op=ALU.add)
 
         def clamp(c, lo=0, hi=TILES):
             nc.vector.tensor_scalar(
                 out=recon[c][:, lo:hi, :],
                 in0=logit[c][:, lo:hi, :],
-                scalar1=-CLAMP,
-                scalar2=-1.0,
-                op0=ALU.min,
-                op1=ALU.mult,
+                scalar1=CLAMP,
+                scalar2=-CLAMP,
+                op0=ALU.max,
+                op1=ALU.add,
+            )
+
+        def on_scalar(j):
+            return j % TILES == 0 and j // TILES >= SLO
+
+        def clamp_scalar(j):
+            c, r = divmod(j, TILES)
+            nc.scalar.activation(
+                out=recon[c][:, r, :],
+                in_=logit[c][:, r, :],
+                func=ACT.Relu,
+                bias=up[:],
+                scale=1.0,
+                accum_out=sum_rl[:, c : c + 1],
             )
 
         def fold(c, rs=(0, 1, 2, 3)):
@@ -221,10 +235,11 @@ def tile_vae_pb_t_kernel(tc, h_dec0, x, dw1, db1, dw2, db2, out_0, out_1):
                 pool, tag = (ps_t, "xt") if c // 2 % 2 == 0 else (ps_z, "z")
                 sums[c] = pool.tile([P, TILES, P], F32, name="sums%d" % c, tag=tag)
             for r in rs:
-                if r in WARM:
+                if on_scalar(TILES * c + r):
+                    continue
+                if (r == 1 and on_scalar(TILES * c) and 0 in WARM) or r in WARM:
                     free = sums[c][:, r:, :].rearrange("p r n -> p (r n)")
                     nc.tensor.matmul(out=free, lhsT=ones[:], rhs=brow[:, : P * (TILES - r)], start=True, stop=True)
-                last = not on_gpsimd(TILES * c + r)
                 for b in range(4):
                     nc.tensor.matmul(
                         out=sums[c][:, r, :],
@@ -232,32 +247,8 @@ def tile_vae_pb_t_kernel(tc, h_dec0, x, dw1, db1, dw2, db2, out_0, out_1):
                         rhs=ident[:],
                         is_transpose=True,
                         start=b == 0,
-                        stop=last and b == 3,
+                        stop=b == 3,
                     )
-
-        def on_gpsimd(j):
-            return j in PRODUCTS
-
-        def product(j):
-            c, r = divmod(j, TILES)
-            nc.gpsimd.tensor_tensor(
-                out=logit[c][:, r, :],
-                in0=logit[c][:, r, :],
-                in1=xs[c][:, WIDTH * r : WIDTH * (r + 1)],
-                op=ALU.mult,
-            )
-
-        def fold_product(j):
-            c, r = divmod(j, TILES)
-            for b in range(4):
-                nc.tensor.matmul(
-                    out=sums[c][:, r, :],
-                    lhsT=logit[c][:, r, P * b : P * (b + 1)],
-                    rhs=ident[:],
-                    is_transpose=True,
-                    start=False,
-                    stop=b == 3,
-                )
 
         def unload(c, on_vector=False):
             if c % 2 == 0:
@@ -267,13 +258,16 @@ def tile_vae_pb_t_kernel(tc, h_dec0, x, dw1, db1, dw2, db2, out_0, out_1):
                     pair = work.tile([P, 2, TILES, P], F32, name="pair%d" % c, tag="g1", align_bytes=64)
                 halves[c] = pair
                 halves[c + 1] = pair
+            lo = 1 if on_scalar(TILES * c) else 0
             if on_vector:
-                nc.vector.tensor_copy(out=halves[c][:, c % 2, :, :], in_=sums[c][:])
+                nc.vector.tensor_copy(out=halves[c][:, c % 2, lo:, :], in_=sums[c][:, lo:, :])
             else:
-                nc.scalar.copy(out=halves[c][:, c % 2, :, :], in_=sums[c][:])
+                nc.scalar.copy(out=halves[c][:, c % 2, lo:, :], in_=sums[c][:, lo:, :])
 
         def total(c):
             for r in range(TILES):
+                if on_scalar(TILES * c + r):
+                    continue
                 nc.tensor.matmul(
                     out=totals[:, TILES * c + r : TILES * c + r + 1],
                     lhsT=halves[c][:, c % 2, r, :],
@@ -284,7 +278,7 @@ def tile_vae_pb_t_kernel(tc, h_dec0, x, dw1, db1, dw2, db2, out_0, out_1):
 
         def sigmoid_store(c, lo=0, hi=CW):
             flat = recon[c][:].rearrange("p r k -> p (r k)")[:, lo:hi]
-            nc.scalar.activation(out=flat, in_=flat, func=ACT.Sigmoid)
+            nc.scalar.activation(out=flat, in_=flat, func=ACT.Sigmoid, bias=down[:], scale=1.0)
             nc.sync.dma_start(out=o_rows[:, CW * c + lo : CW * c + hi], in_=flat)
 
         def pair(c):
@@ -315,8 +309,6 @@ def tile_vae_pb_t_kernel(tc, h_dec0, x, dw1, db1, dw2, db2, out_0, out_1):
         def dot_x(n):
             for j in range(state["dots"], min(ROWS, state["dots"] + n)):
                 c, r = divmod(j, TILES)
-                if on_gpsimd(j):
-                    continue
                 nc.vector.scalar_tensor_tensor(
                     out=logit[c][:, r, :],
                     in0=logit[c][:, r, :],
@@ -334,7 +326,8 @@ def tile_vae_pb_t_kernel(tc, h_dec0, x, dw1, db1, dw2, db2, out_0, out_1):
         nc.gpsimd.memset(warm[:], 0.0)
         nc.scalar.activation(out=warm[:], in_=warm[:], func=ACT.Silu)
         nc.vector.memset(onesf[:], 1.0)
-        nc.vector.memset(sum_lx[:], 0.0)
+        nc.vector.memset(up[:], -CLAMP)
+        nc.vector.memset(down[:], CLAMP)
         make_identity(nc, ident[:])
         nc.gpsimd.memset(ones[:], 1.0)
         h0[0] = io.tile([P, CW], BF16, name="h0_0", tag="io")
@@ -455,19 +448,14 @@ def tile_vae_pb_t_kernel(tc, h_dec0, x, dw1, db1, dw2, db2, out_0, out_1):
 
         halves_done = set()
         for c in range(CHUNKS):
-            before = [j for j in range(TILES * (c - 1), TILES * c) if j in PRODUCTS]
-            for j in before:
-                product(j)
             if c >= state["clamped"]:
                 add_some(min(ROWS, TILES * (c + 1) + AHEAD) - state["added"], DEEP, ROWS)
                 if c < CHUNKS - 1:
-                    clamp(c)
+                    clamp(c, 1 if on_scalar(TILES * c) else 0)
                 state["clamped"] += 1
-            for j in before:
-                fold_product(j)
             if c == CHUNKS - 1:
                 for lo in (0, 2):
-                    clamp(c, lo, lo + 2)
+                    clamp(c, 1 if lo == 0 and on_scalar(TILES * c) else lo, lo + 2)
                     fold(c, (lo, lo + 1))
                     sigmoid_store(c, WIDTH * lo, WIDTH * (lo + 2))
             if c >= VLAG:
@@ -476,15 +464,14 @@ def tile_vae_pb_t_kernel(tc, h_dec0, x, dw1, db1, dw2, db2, out_0, out_1):
                 if c not in sums:
                     fold(c)
                 sigmoid_store(c)
-            if c >= ULAG and c - ULAG not in UV:
-                unload(c - ULAG)
+            if c + 1 < CHUNKS and on_scalar(TILES * (c + 1)):
+                clamp_scalar(TILES * (c + 1))
+            if c not in UV:
+                unload(c)
             if c >= DFROM:
                 dot_x(DOTS)
         for c in range(CHUNKS):
             unload_v(c)
-        for c in range(CHUNKS - ULAG, CHUNKS):
-            if c not in UV:
-                unload(c)
         totals = ps_a.tile([P, ROWS], F32, name="totals", tag="acc")
         for c in range(CHUNKS):
             total(c)
@@ -493,6 +480,23 @@ def tile_vae_pb_t_kernel(tc, h_dec0, x, dw1, db1, dw2, db2, out_0, out_1):
             pair(c)
             log_sum(c)
 
-        nc.vector.tensor_tensor(out=part[:], in0=totals[:], in1=sum_lx[:], op=ALU.add)
+        def by_tile(t):
+            return t.rearrange("p (c r) -> p c r", r=TILES)
+
+        def finish(rows, total_of_rows):
+            nc.vector.scalar_tensor_tensor(
+                out=rows(by_tile(part[:])),
+                in0=total_of_rows,
+                scalar=CLAMP * WIDTH,
+                in1=rows(by_tile(sum_lx[:])),
+                op0=ALU.add,
+                op1=ALU.subtract,
+            )
+
+        finish(lambda t: t[:, :, 1:], by_tile(totals[:])[:, :, 1:])
+        if SLO > 0:
+            finish(lambda t: t[:, :SLO, 0], by_tile(totals[:])[:, :SLO, 0])
+        if SLO < CHUNKS:
+            finish(lambda t: t[:, SLO:, 0], sum_rl[:, SLO:])
         nc.vector.tensor_tensor(out=bce[:], in0=part[:], in1=sum_ln[:], op=ALU.subtract)
         nc.sync.dma_start(out=out_0.rearrange("(p q) -> p q", q=ROWS), in_=bce[:])

@@ -22,21 +22,28 @@ CW = TILES * WIDTH
 CLAMP = -40.0
 BIAS_S = False
 VLAG = 8
+NTAIL = 6
+NCL = 2
+NC1 = 4
+HEADT = 0
+HEADQ = 0
+EVV = ()
+Q0F = ()
 TPOS = 1
 LAP = 8
-GCOLS = (0, 0, 288, 288, 288, 288, 288, 288)
+GCOLS = (0, 0, 208, 208, 208, 208, 208, 208)
 ADDS = (0, 0, 3, 3, 3, 3, 3, 3)
 CL = (0, 0, 0, 0, 1, 1, 0, 0)
-UV = (4, 5, 6, 7)
+UV = ()
 FOLDS = (0, 0, 0, 0, 0, 0, 1, 1)
 AHEAD = 1
 DOTS = 0
 DFROM = 3
 LOOK = 2
 DEEP = 4
-NPAIR = (0, 0, 0, 0, 0, 0, 4, 4)
-SLO = 2
-WARM = (0,)
+NPAIR = (0, 0, 0, 0, 0, 0, 0, 2)
+SLO = 8
+WARM = ()
 FIRST_LATE = sum(ADDS)
 
 
@@ -75,12 +82,12 @@ def tile_vae_pb_t_kernel(tc, h_dec0, x, dw1, db1, dw2, db2, out_0, out_1):
         warm = const.tile([P, 1], F32, name="warm")
         part = const.tile([P, ROWS], F32, name="part")
         bce = const.tile([P, ROWS], F32, name="bce")
-        junk = const.tile([P, 2 * TILES, WIDTH], BF16, name="junk")
+        junk = const.tile([P, TILES, WIDTH], BF16, name="junk")
         logit = [const.tile([P, TILES, WIDTH], F32, name="logit%d" % c) for c in range(CHUNKS)]
         recon = [const.tile([P, TILES, WIDTH], F32, name="recon%d" % c) for c in range(CHUNKS)]
-        c1 = [const.tile([P, WIDTH], U32, name="c1_%d" % c, align_bytes=64) for c in range(CHUNKS)]
-        s1 = [const.tile([P, WIDTH], U8, name="s1_%d" % c, align_bytes=64) for c in range(CHUNKS)]
-
+        c1 = {}
+        s1 = {}
+        tail = {}
         h0 = {}
         xs = {}
         xts = {}
@@ -105,22 +112,25 @@ def tile_vae_pb_t_kernel(tc, h_dec0, x, dw1, db1, dw2, db2, out_0, out_1):
         def transposes(c, bs=(0, 1)):
             words = h0[c][:].bitcast(F32)
             for b in bs:
-                xt = ps_t.tile([P, 2, 256], F32, name="xt%d_%d" % (c, b), tag="xt")
+                pool, tag = (ps_a, "acc") if c == 1 else (ps_t, "xt")
+                xt = pool.tile([P, 2, 256], F32, name="xt%d_%d" % (c, b), tag=tag)
                 for r2 in range(2):
                     for u in range(2):
                         lo = 256 * (2 * b + r2) + P * u
                         nc.tensor.transpose(xt[:, u, P * r2 : P * (r2 + 1)], words[:, lo : lo + P], ident[:])
                 xts[(c, b)] = xt
 
-        def evacuate(c, bs=(0, 1)):
-            if 0 in bs:
+        def evacuate(c, bs=(0, 1), on_vector=False):
+            if c not in g0:
                 g0[c] = work.tile([P, CW], BF16, name="g0_%d" % c, tag="g0", bufs=LOOK, align_bytes=64)
             pairs = g0[c][:].bitcast(F32).rearrange("p (w u) -> p w u", u=2)
             for b in bs:
-                nc.scalar.copy(
-                    out=pairs[:, 256 * b : 256 * (b + 1), :],
-                    in_=xts[(c, b)][:].rearrange("p u w -> p w u"),
-                )
+                out = pairs[:, 256 * b : 256 * (b + 1), :]
+                in_ = xts[(c, b)][:].rearrange("p u w -> p w u")
+                if on_vector:
+                    nc.vector.tensor_copy(out=out, in_=in_)
+                else:
+                    nc.scalar.copy(out=out, in_=in_)
 
         def quantise0(c, lo=0, hi=WIDTH):
             if lo == 0:
@@ -179,6 +189,8 @@ def tile_vae_pb_t_kernel(tc, h_dec0, x, dw1, db1, dw2, db2, out_0, out_1):
                 )
 
         def quantise1(c):
+            c1[c] = work.tile([P, WIDTH], U32, name="c1_%d" % c, tag="c1", bufs=NC1, align_bytes=64)
+            s1[c] = work.tile([P, WIDTH], U8, name="s1_%d" % c, tag="s1", bufs=NC1, align_bytes=64)
             nc.vector.quantize_mx(
                 out=c1[c][:].bitcast(FP8X4), scales=s1[c][:], in_=g1[c][:].rearrange("p w t -> p (w t)")
             )
@@ -206,9 +218,16 @@ def tile_vae_pb_t_kernel(tc, h_dec0, x, dw1, db1, dw2, db2, out_0, out_1):
             c, r = divmod(j, TILES)
             nc.vector.tensor_tensor(out=logit[c][:, r, :], in0=accs[j][:], in1=b2bc[:], op=ALU.add)
 
+        def clamped(c):
+            if c < CHUNKS - NTAIL:
+                return recon[c]
+            if c not in tail:
+                tail[c] = work.tile([P, TILES, WIDTH], F32, name="cl%d" % c, tag="cl", bufs=NCL)
+            return tail[c]
+
         def clamp(c, lo=0, hi=TILES):
             nc.vector.tensor_scalar(
-                out=recon[c][:, lo:hi, :],
+                out=clamped(c)[:, lo:hi, :],
                 in0=logit[c][:, lo:hi, :],
                 scalar1=CLAMP,
                 scalar2=-CLAMP,
@@ -222,7 +241,7 @@ def tile_vae_pb_t_kernel(tc, h_dec0, x, dw1, db1, dw2, db2, out_0, out_1):
         def clamp_scalar(j):
             c, r = divmod(j, TILES)
             nc.scalar.activation(
-                out=recon[c][:, r, :],
+                out=clamped(c)[:, r, :],
                 in_=logit[c][:, r, :],
                 func=ACT.Relu,
                 bias=up[:],
@@ -243,7 +262,7 @@ def tile_vae_pb_t_kernel(tc, h_dec0, x, dw1, db1, dw2, db2, out_0, out_1):
                 for b in range(4):
                     nc.tensor.matmul(
                         out=sums[c][:, r, :],
-                        lhsT=recon[c][:, r, P * b : P * (b + 1)],
+                        lhsT=clamped(c)[:, r, P * b : P * (b + 1)],
                         rhs=ident[:],
                         is_transpose=True,
                         start=b == 0,
@@ -278,7 +297,8 @@ def tile_vae_pb_t_kernel(tc, h_dec0, x, dw1, db1, dw2, db2, out_0, out_1):
 
         def sigmoid_store(c, lo=0, hi=CW):
             flat = recon[c][:].rearrange("p r k -> p (r k)")[:, lo:hi]
-            nc.scalar.activation(out=flat, in_=flat, func=ACT.Sigmoid, bias=down[:], scale=1.0)
+            source = clamped(c)[:].rearrange("p r k -> p (r k)")[:, lo:hi]
+            nc.scalar.activation(out=flat, in_=source, func=ACT.Sigmoid, bias=down[:], scale=1.0)
             nc.sync.dma_start(out=o_rows[:, CW * c + lo : CW * c + hi], in_=flat)
 
         def pair(c):
@@ -296,14 +316,14 @@ def tile_vae_pb_t_kernel(tc, h_dec0, x, dw1, db1, dw2, db2, out_0, out_1):
                 j = TILES * c + r
                 if r >= TILES - NPAIR[c]:
                     nc.scalar.activation(
-                        out=junk[:, j % (2 * TILES), : WIDTH // 2],
+                        out=junk[:, j % TILES, : WIDTH // 2],
                         in_=logit[c][:, r, : WIDTH // 2],
                         func=ACT.Ln,
                         accum_out=sum_ln[:, j : j + 1],
                     )
                     continue
                 nc.scalar.activation(
-                    out=junk[:, j % (2 * TILES), :], in_=recon[c][:, r, :], func=ACT.Ln, accum_out=sum_ln[:, j : j + 1]
+                    out=junk[:, j % TILES, :], in_=recon[c][:, r, :], func=ACT.Ln, accum_out=sum_ln[:, j : j + 1]
                 )
 
         def dot_x(n):
@@ -373,18 +393,24 @@ def tile_vae_pb_t_kernel(tc, h_dec0, x, dw1, db1, dw2, db2, out_0, out_1):
         quant1(3)
         transposes(0, (1,))
         evacuate(0, (1,))
+        if HEADT == 0:
+            transposes(1)
         layer1(0, 0, half_w)
         silu(0, 0, half_w)
-        transposes(1)
-        evacuate(1)
         quantise0(0, half_w, WIDTH)
         layer1(0, half_w, WIDTH)
+        if HEADT == 1:
+            transposes(1)
+        evacuate(1, on_vector=True)
+        if HEADQ == 0:
+            quantise0(1)
         wg2 = work.tile([P, CW], BF16, name="wg2", tag="g1", align_bytes=64)
         nc.vector.tensor_copy(
             out=wg2[:].rearrange("p (c i t) -> p c t i", i=4, t=4),
             in_=raw2[:].rearrange("p (t c i) -> p c t i", t=4, i=4),
         )
-        quantise0(1)
+        if HEADQ == 1:
+            quantise0(1)
         nc.vector.quantize_mx(out=w2c[:].bitcast(FP8X4), scales=w2s[:], in_=wg2[:])
 
         transposes(LOOK)
@@ -409,7 +435,7 @@ def tile_vae_pb_t_kernel(tc, h_dec0, x, dw1, db1, dw2, db2, out_0, out_1):
             else:
                 silu(c)
             if c + LOOK < CHUNKS:
-                evacuate(c + LOOK)
+                evacuate(c + LOOK, tuple(b for b in (0, 1) if 2 * (c + LOOK) + b not in EVV))
             load_x(c)
             if c + 1 < CHUNKS:
                 layer1(c + 1)
@@ -423,12 +449,16 @@ def tile_vae_pb_t_kernel(tc, h_dec0, x, dw1, db1, dw2, db2, out_0, out_1):
             n = min(ADDS[c], TILES * c - state["added"])
             stop = TILES * c
             issue(min(stop - state["issued"], 2 - (state["issued"] - state["added"])))
+            if c in Q0F:
+                quantise0(c + LOOK)
             regroup(c)
             add_some(n, 2, stop)
             if c + LOOK + 1 < CHUNKS and TPOS == 1:
                 transposes(c + LOOK + 1)
             if c + LOOK < CHUNKS:
-                quantise0(c + LOOK)
+                evacuate(c + LOOK, tuple(b for b in (0, 1) if 2 * (c + LOOK) + b in EVV), True)
+                if c not in Q0F:
+                    quantise0(c + LOOK)
             quantise1(c)
             if c == 0:
                 if BIAS_S:

@@ -19,32 +19,18 @@ ROWS = BATCH // P
 TILES = 4
 CHUNKS = ROWS // TILES
 CW = TILES * WIDTH
+HALF = WIDTH // 2
 CLAMP = -40.0
-BIAS_S = False
-VLAG = 8
-NTAIL = 6
-NCL = 2
-NC1 = 4
-HEADT = 0
-HEADQ = 0
-EVV = ()
-Q0F = ()
-TPOS = 1
-LAP = 8
-GCOLS = (0, 0, 208, 208, 208, 208, 208, 208)
-ADDS = (0, 0, 3, 3, 3, 3, 3, 3)
-CL = (0, 0, 0, 0, 1, 1, 0, 0)
-UV = ()
-FOLDS = (0, 0, 0, 0, 0, 0, 1, 1)
-AHEAD = 1
-DOTS = 0
-DFROM = 3
 LOOK = 2
+GROUPED_BY_GPSIMD = 208
+LAP = 8
+ADDS = 3
+FIRST_ADDS = 2
+EARLY_CLAMPS = (4, 5)
+EARLY_FOLDS = (6, 7)
+EARLY = len(EARLY_CLAMPS)
 DEEP = 4
-NPAIR = (0, 0, 0, 0, 0, 0, 0, 2)
-SLO = 8
-WARM = ()
-FIRST_LATE = sum(ADDS)
+PAIRED = CHUNKS - 2
 
 
 def tile_vae_pb_t_kernel(tc, h_dec0, x, dw1, db1, dw2, db2, out_0, out_1):
@@ -76,30 +62,16 @@ def tile_vae_pb_t_kernel(tc, h_dec0, x, dw1, db1, dw2, db2, out_0, out_1):
         sum_lx = const.tile([P, ROWS], F32, name="sum_lx")
         sum_ln = const.tile([P, ROWS], F32, name="sum_ln")
         onesf = const.tile([P, 1], F32, name="onesf")
-        up = const.tile([P, 1], F32, name="up")
-        down = const.tile([P, 1], F32, name="down")
-        sum_rl = const.tile([P, CHUNKS], F32, name="sum_rl")
         warm = const.tile([P, 1], F32, name="warm")
         part = const.tile([P, ROWS], F32, name="part")
         bce = const.tile([P, ROWS], F32, name="bce")
-        junk = const.tile([P, TILES, WIDTH], BF16, name="junk")
+        unread = const.tile([P, 2, WIDTH], BF16, name="unread")
         logit = [const.tile([P, TILES, WIDTH], F32, name="logit%d" % c) for c in range(CHUNKS)]
         recon = [const.tile([P, TILES, WIDTH], F32, name="recon%d" % c) for c in range(CHUNKS)]
-        c1 = {}
-        s1 = {}
-        tail = {}
-        h0 = {}
-        xs = {}
-        xts = {}
-        g0 = {}
-        c0 = {}
-        s0 = {}
-        zs = {}
-        hs = {}
-        g1 = {}
-        accs = {}
-        sums = {}
-        halves = {}
+
+        h0, xs, xts, g0, c0, s0 = {}, {}, {}, {}, {}, {}
+        zs, hs, g1, c1, s1 = {}, {}, {}, {}, {}
+        accs, clamped, sums, halves = {}, {}, {}, {}
 
         def load_h(c):
             h0[c] = io.tile([P, CW], BF16, name="h0_%d" % c, tag="io")
@@ -109,10 +81,9 @@ def tile_vae_pb_t_kernel(tc, h_dec0, x, dw1, db1, dw2, db2, out_0, out_1):
             xs[c] = io.tile([P, CW], BF16, name="x_%d" % c, tag="io")
             nc.sync.dma_start(out=xs[c][:], in_=x_rows[:, CW * c : CW * (c + 1)])
 
-        def transposes(c, bs=(0, 1)):
+        def transposes(c, bs=(0, 1), pool=ps_t, tag="xt"):
             words = h0[c][:].bitcast(F32)
             for b in bs:
-                pool, tag = (ps_a, "acc") if c == 1 else (ps_t, "xt")
                 xt = pool.tile([P, 2, 256], F32, name="xt%d_%d" % (c, b), tag=tag)
                 for r2 in range(2):
                     for u in range(2):
@@ -120,17 +91,12 @@ def tile_vae_pb_t_kernel(tc, h_dec0, x, dw1, db1, dw2, db2, out_0, out_1):
                         nc.tensor.transpose(xt[:, u, P * r2 : P * (r2 + 1)], words[:, lo : lo + P], ident[:])
                 xts[(c, b)] = xt
 
-        def evacuate(c, bs=(0, 1), on_vector=False):
+        def evacuate(copy, c, bs=(0, 1)):
             if c not in g0:
                 g0[c] = work.tile([P, CW], BF16, name="g0_%d" % c, tag="g0", bufs=LOOK, align_bytes=64)
-            pairs = g0[c][:].bitcast(F32).rearrange("p (w u) -> p w u", u=2)
+            words = g0[c][:].bitcast(F32).rearrange("p (w u) -> p w u", u=2)
             for b in bs:
-                out = pairs[:, 256 * b : 256 * (b + 1), :]
-                in_ = xts[(c, b)][:].rearrange("p u w -> p w u")
-                if on_vector:
-                    nc.vector.tensor_copy(out=out, in_=in_)
-                else:
-                    nc.scalar.copy(out=out, in_=in_)
+                copy(out=words[:, 256 * b : 256 * (b + 1), :], in_=xts[(c, b)][:].rearrange("p u w -> p w u"))
 
         def quantise0(c, lo=0, hi=WIDTH):
             if lo == 0:
@@ -159,25 +125,20 @@ def tile_vae_pb_t_kernel(tc, h_dec0, x, dw1, db1, dw2, db2, out_0, out_1):
 
         def silu(c, lo=0, hi=WIDTH):
             if lo == 0:
-                hs[c] = work.tile([P, 4, WIDTH], BF16, name="hs%d" % c, tag="hs")
+                hs[c] = work.tile([P, 4, WIDTH], BF16, name="hs%d" % c, tag="hs", align_bytes=64)
             for t in (1, 0, 3, 2):
                 nc.scalar.activation(
-                    out=hs[c][:, t, lo:hi],
-                    in_=zs[(c, lo, t)],
-                    func=ACT.Silu,
-                    bias=b1f[:, t : t + 1],
-                    scale=1.0,
+                    out=hs[c][:, t, lo:hi], in_=zs[(c, lo, t)], func=ACT.Silu, bias=b1f[:, t : t + 1], scale=1.0
                 )
 
         def regroup(c):
             g1[c] = work.tile([P, WIDTH, 4], BF16, name="g1_%d" % c, tag="g1", align_bytes=64)
-            cut = WIDTH - GCOLS[c]
+            cut = WIDTH - GROUPED_BY_GPSIMD if c >= FIRST_ADDS else WIDTH
             own = min(WIDTH, cut + LAP)
-            if cut > 0:
-                nc.vector.tensor_copy(
-                    out=g1[c][:, :own, :].rearrange("p (c i) t -> p c t i", i=4),
-                    in_=hs[c][:, :, :own].rearrange("p t (c i) -> p c t i", i=4),
-                )
+            nc.vector.tensor_copy(
+                out=g1[c][:, :own, :].rearrange("p (c i) t -> p c t i", i=4),
+                in_=hs[c][:, :, :own].rearrange("p t (c i) -> p c t i", i=4),
+            )
             if cut < WIDTH:
                 nc.gpsimd.tensor_scalar(
                     out=g1[c][:, cut:, :],
@@ -189,20 +150,16 @@ def tile_vae_pb_t_kernel(tc, h_dec0, x, dw1, db1, dw2, db2, out_0, out_1):
                 )
 
         def quantise1(c):
-            c1[c] = work.tile([P, WIDTH], U32, name="c1_%d" % c, tag="c1", bufs=NC1, align_bytes=64)
-            s1[c] = work.tile([P, WIDTH], U8, name="s1_%d" % c, tag="s1", bufs=NC1, align_bytes=64)
+            c1[c] = work.tile([P, WIDTH], U32, name="c1_%d" % c, tag="c1", bufs=4, align_bytes=64)
+            s1[c] = work.tile([P, WIDTH], U8, name="s1_%d" % c, tag="s1", bufs=4, align_bytes=64)
             nc.vector.quantize_mx(
                 out=c1[c][:].bitcast(FP8X4), scales=s1[c][:], in_=g1[c][:].rearrange("p w t -> p (w t)")
             )
 
         def layer2(j):
-            if j >= ROWS:
-                return
             c, r = divmod(j, TILES)
-            if j >= FIRST_LATE + 2 and j // 2 % 2 == 0:
-                acc = ps_y.tile([P, WIDTH], F32, name="acc%d" % j, tag="y")
-            else:
-                acc = ps_a.tile([P, WIDTH], F32, name="acc%d" % j, tag="acc")
+            pool, tag = (ps_y, "y") if j in in_y else (ps_a, "acc")
+            acc = pool.tile([P, WIDTH], F32, name="acc%d" % j, tag=tag)
             nc.tensor.matmul_mx(
                 out=acc[:],
                 lhsT=c1[c][:, P * r : P * (r + 1)].bitcast(FP8X4),
@@ -218,75 +175,39 @@ def tile_vae_pb_t_kernel(tc, h_dec0, x, dw1, db1, dw2, db2, out_0, out_1):
             c, r = divmod(j, TILES)
             nc.vector.tensor_tensor(out=logit[c][:, r, :], in0=accs[j][:], in1=b2bc[:], op=ALU.add)
 
-        def clamped(c):
-            if c < CHUNKS - NTAIL:
-                return recon[c]
-            if c not in tail:
-                tail[c] = work.tile([P, TILES, WIDTH], F32, name="cl%d" % c, tag="cl", bufs=NCL)
-            return tail[c]
-
         def clamp(c, lo=0, hi=TILES):
+            if c not in clamped:
+                if c < EARLY:
+                    clamped[c] = recon[c]
+                else:
+                    clamped[c] = work.tile([P, TILES, WIDTH], F32, name="clamped%d" % c, tag="clamped", bufs=3)
             nc.vector.tensor_scalar(
-                out=clamped(c)[:, lo:hi, :],
-                in0=logit[c][:, lo:hi, :],
-                scalar1=CLAMP,
-                scalar2=-CLAMP,
-                op0=ALU.max,
-                op1=ALU.add,
+                out=clamped[c][:, lo:hi, :], in0=logit[c][:, lo:hi, :], scalar1=CLAMP, scalar2=None, op0=ALU.max
             )
 
-        def on_scalar(j):
-            return j % TILES == 0 and j // TILES >= SLO
-
-        def clamp_scalar(j):
-            c, r = divmod(j, TILES)
-            nc.scalar.activation(
-                out=clamped(c)[:, r, :],
-                in_=logit[c][:, r, :],
-                func=ACT.Relu,
-                bias=up[:],
-                scale=1.0,
-                accum_out=sum_rl[:, c : c + 1],
-            )
-
-        def fold(c, rs=(0, 1, 2, 3)):
-            if 0 in rs:
-                pool, tag = (ps_t, "xt") if c // 2 % 2 == 0 else (ps_z, "z")
-                sums[c] = pool.tile([P, TILES, P], F32, name="sums%d" % c, tag=tag)
-            for r in rs:
-                if on_scalar(TILES * c + r):
-                    continue
-                if (r == 1 and on_scalar(TILES * c) and 0 in WARM) or r in WARM:
-                    free = sums[c][:, r:, :].rearrange("p r n -> p (r n)")
-                    nc.tensor.matmul(out=free, lhsT=ones[:], rhs=brow[:, : P * (TILES - r)], start=True, stop=True)
+        def fold(c):
+            pool, tag = (ps_t, "xt") if c // 2 % 2 == 0 else (ps_z, "z")
+            sums[c] = pool.tile([P, TILES, P], F32, name="sums%d" % c, tag=tag)
+            for r in range(TILES):
                 for b in range(4):
                     nc.tensor.matmul(
                         out=sums[c][:, r, :],
-                        lhsT=clamped(c)[:, r, P * b : P * (b + 1)],
+                        lhsT=clamped[c][:, r, P * b : P * (b + 1)],
                         rhs=ident[:],
                         is_transpose=True,
                         start=b == 0,
                         stop=b == 3,
                     )
 
-        def unload(c, on_vector=False):
+        def unload(c):
             if c % 2 == 0:
-                if c < 4:
-                    pair = work.tile([P, 2, TILES, P], F32, name="pair%d" % c, tag="hs")
-                else:
-                    pair = work.tile([P, 2, TILES, P], F32, name="pair%d" % c, tag="g1", align_bytes=64)
-                halves[c] = pair
-                halves[c + 1] = pair
-            lo = 1 if on_scalar(TILES * c) else 0
-            if on_vector:
-                nc.vector.tensor_copy(out=halves[c][:, c % 2, lo:, :], in_=sums[c][:, lo:, :])
-            else:
-                nc.scalar.copy(out=halves[c][:, c % 2, lo:, :], in_=sums[c][:, lo:, :])
+                tag = "hs" if c < 4 else "g1"
+                halves[c] = work.tile([P, 2, TILES, P], F32, name="halves%d" % c, tag=tag, align_bytes=64)
+                halves[c + 1] = halves[c]
+            nc.scalar.copy(out=halves[c][:, c % 2, :, :], in_=sums[c][:])
 
         def total(c):
             for r in range(TILES):
-                if on_scalar(TILES * c + r):
-                    continue
                 nc.tensor.matmul(
                     out=totals[:, TILES * c + r : TILES * c + r + 1],
                     lhsT=halves[c][:, c % 2, r, :],
@@ -295,50 +216,32 @@ def tile_vae_pb_t_kernel(tc, h_dec0, x, dw1, db1, dw2, db2, out_0, out_1):
                     stop=True,
                 )
 
-        def sigmoid_store(c, lo=0, hi=CW):
-            flat = recon[c][:].rearrange("p r k -> p (r k)")[:, lo:hi]
-            source = clamped(c)[:].rearrange("p r k -> p (r k)")[:, lo:hi]
-            nc.scalar.activation(out=flat, in_=source, func=ACT.Sigmoid, bias=down[:], scale=1.0)
-            nc.sync.dma_start(out=o_rows[:, CW * c + lo : CW * c + hi], in_=flat)
+        def sigmoid_store(c, lo=0, hi=TILES):
+            nc.scalar.activation(out=recon[c][:, lo:hi, :], in_=clamped[c][:, lo:hi, :], func=ACT.Sigmoid)
+            nc.sync.dma_start(
+                out=o_rows[:, CW * c + WIDTH * lo : CW * c + WIDTH * hi],
+                in_=recon[c][:, lo:hi, :].rearrange("p r k -> p (r k)"),
+            )
 
-        def pair(c):
-            n = NPAIR[c]
-            if n > 0:
-                nc.vector.tensor_tensor(
-                    out=logit[c][:, TILES - n :, : WIDTH // 2],
-                    in0=recon[c][:, TILES - n :, : WIDTH // 2],
-                    in1=recon[c][:, TILES - n :, WIDTH // 2 :],
-                    op=ALU.mult,
-                )
+        def log_sum(j):
+            c, r = divmod(j, TILES)
+            source = products[:, r, :] if c == PAIRED else recon[c][:, r, :]
+            width = HALF if c == PAIRED else WIDTH
+            nc.scalar.activation(
+                out=unread[:, j % 2, :width], in_=source, func=ACT.Ln, accum_out=sum_ln[:, j : j + 1]
+            )
 
-        def log_sum(c):
-            for r in range(TILES):
-                j = TILES * c + r
-                if r >= TILES - NPAIR[c]:
-                    nc.scalar.activation(
-                        out=junk[:, j % TILES, : WIDTH // 2],
-                        in_=logit[c][:, r, : WIDTH // 2],
-                        func=ACT.Ln,
-                        accum_out=sum_ln[:, j : j + 1],
-                    )
-                    continue
-                nc.scalar.activation(
-                    out=junk[:, j % TILES, :], in_=recon[c][:, r, :], func=ACT.Ln, accum_out=sum_ln[:, j : j + 1]
-                )
-
-        def dot_x(n):
-            for j in range(state["dots"], min(ROWS, state["dots"] + n)):
-                c, r = divmod(j, TILES)
-                nc.vector.scalar_tensor_tensor(
-                    out=logit[c][:, r, :],
-                    in0=logit[c][:, r, :],
-                    scalar=1.0,
-                    in1=xs[c][:, WIDTH * r : WIDTH * (r + 1)],
-                    op0=ALU.mult,
-                    op1=ALU.mult,
-                    accum_out=sum_lx[:, j : j + 1],
-                )
-            state["dots"] = min(ROWS, state["dots"] + n)
+        def dot_x(j):
+            c, r = divmod(j, TILES)
+            nc.vector.scalar_tensor_tensor(
+                out=logit[c][:, r, :],
+                in0=logit[c][:, r, :],
+                scalar=1.0,
+                in1=xs[c][:, WIDTH * r : WIDTH * (r + 1)],
+                op0=ALU.mult,
+                op1=ALU.mult,
+                accum_out=sum_lx[:, j : j + 1],
+            )
 
         nc.scalar.dma_start(out=b1r[:], in_=db1.rearrange("(p t) -> p t", t=4))
         nc.vector.memset(brow[:], 0.0)
@@ -346,32 +249,29 @@ def tile_vae_pb_t_kernel(tc, h_dec0, x, dw1, db1, dw2, db2, out_0, out_1):
         nc.gpsimd.memset(warm[:], 0.0)
         nc.scalar.activation(out=warm[:], in_=warm[:], func=ACT.Silu)
         nc.vector.memset(onesf[:], 1.0)
-        nc.vector.memset(up[:], -CLAMP)
-        nc.vector.memset(down[:], CLAMP)
         make_identity(nc, ident[:])
         nc.gpsimd.memset(ones[:], 1.0)
         h0[0] = io.tile([P, CW], BF16, name="h0_0", tag="io")
-        half = CW // 2
-        nc.sync.dma_start(out=h0[0][:, :half], in_=h_rows[:, :half])
-        raw1 = work.tile([P, CW], BF16, name="raw1", tag="hs")
+        nc.sync.dma_start(out=h0[0][:, : CW // 2], in_=h_rows[:, : CW // 2])
+        raw1 = work.tile([P, CW], BF16, name="raw1", tag="hs", align_bytes=64)
         nc.sync.dma_start(
             out=raw1[:].rearrange("p (u f) -> p u f", u=2),
             in_=dw1.rearrange("(u p e) n -> p u (e n)", u=2, p=P, e=2),
         )
-        nc.sync.dma_start(out=h0[0][:, half:], in_=h_rows[:, half:CW])
+        nc.sync.dma_start(out=h0[0][:, CW // 2 :], in_=h_rows[:, CW // 2 : CW])
         load_h(1)
-        raw2 = work.tile([P, CW], BF16, name="raw2", tag="hs")
+        raw2 = work.tile([P, CW], BF16, name="raw2", tag="hs", align_bytes=64)
         nc.sync.dma_start(out=raw2[:], in_=dw2.rearrange("(p t) n -> p (t n)", t=4))
         for c in range(2, CHUNKS):
             load_h(c)
 
         nc.vector.tensor_copy(out=b1f[:], in_=b1r[:])
         wg1 = work.tile([P, CW], BF16, name="wg1", tag="g1", align_bytes=64)
-        wide1 = wg1[:].rearrange("p (s m t) -> p s m t", s=4, m=P, t=4)
+        grouped1 = wg1[:].rearrange("p (s m t) -> p s m t", s=4, m=P, t=4)
         rows1 = raw1[:].rearrange("p (t m s) -> p s m t", t=4, m=P, s=4)
 
-        def group1(s):
-            nc.vector.tensor_copy(out=wide1[:, s, :, :], in_=rows1[:, s, :, :])
+        def group1(copy, s):
+            copy(out=grouped1[:, s, :, :], in_=rows1[:, s, :, :])
 
         def quant1(s):
             cols = slice(P * s, P * (s + 1))
@@ -379,154 +279,111 @@ def tile_vae_pb_t_kernel(tc, h_dec0, x, dw1, db1, dw2, db2, out_0, out_1):
                 out=w1c[:, cols].bitcast(FP8X4), scales=w1s[:, cols], in_=wg1[:, 4 * P * s : 4 * P * (s + 1)]
             )
 
-        half_w = WIDTH // 2
         transposes(0, (0,))
-        evacuate(0, (0,))
-        group1(0)
-        group1(1)
+        evacuate(nc.scalar.copy, 0, (0,))
+        group1(nc.vector.tensor_copy, 0)
+        group1(nc.vector.tensor_copy, 1)
         quant1(0)
-        quantise0(0, 0, half_w)
-        group1(2)
+        quantise0(0, 0, HALF)
+        group1(nc.scalar.copy, 2)
         quant1(1)
-        group1(3)
+        group1(nc.scalar.copy, 3)
         quant1(2)
         quant1(3)
         transposes(0, (1,))
-        evacuate(0, (1,))
-        if HEADT == 0:
-            transposes(1)
-        layer1(0, 0, half_w)
-        silu(0, 0, half_w)
-        quantise0(0, half_w, WIDTH)
-        layer1(0, half_w, WIDTH)
-        if HEADT == 1:
-            transposes(1)
-        evacuate(1, on_vector=True)
-        if HEADQ == 0:
-            quantise0(1)
+        evacuate(nc.scalar.copy, 0, (1,))
+        transposes(1, pool=ps_a, tag="acc")
+        layer1(0, 0, HALF)
+        silu(0, 0, HALF)
+        quantise0(0, HALF, WIDTH)
+        layer1(0, HALF, WIDTH)
+        evacuate(nc.vector.tensor_copy, 1)
+        quantise0(1)
         wg2 = work.tile([P, CW], BF16, name="wg2", tag="g1", align_bytes=64)
         nc.vector.tensor_copy(
-            out=wg2[:].rearrange("p (c i t) -> p c t i", i=4, t=4),
-            in_=raw2[:].rearrange("p (t c i) -> p c t i", t=4, i=4),
+            out=wg2[:].rearrange("p (c i t) -> p c t i", i=4, t=4), in_=raw2[:].rearrange("p (t c i) -> p c t i", t=4, i=4)
         )
-        if HEADQ == 1:
-            quantise0(1)
         nc.vector.quantize_mx(out=w2c[:].bitcast(FP8X4), scales=w2s[:], in_=wg2[:])
-
         transposes(LOOK)
-        state = {"added": 0, "issued": 0, "clamped": 0, "dots": 0}
 
-        def issue(n):
-            for k in range(n):
-                if state["issued"] < ROWS:
-                    layer2(state["issued"])
-                    state["issued"] += 1
+        late = ADDS * (CHUNKS - FIRST_ADDS) + 2
+        in_y = [j for j in range(late, ROWS) if (j - late) // 2 % 2 == 0]
+        state = {"added": 0, "issued": 0}
 
-        def add_some(n, depth, stop):
-            for k in range(n):
+        def issue(depth, ready):
+            while state["issued"] < min(ready, state["added"] + depth):
+                layer2(state["issued"])
+                state["issued"] += 1
+
+        def add_up_to(end, depth, ready):
+            while state["added"] < end:
                 add_bias(state["added"])
                 state["added"] += 1
-                if state["issued"] - state["added"] < depth and state["issued"] < stop:
-                    issue(1)
+                issue(depth, ready)
 
         for c in range(CHUNKS):
             if c == 0:
-                silu(0, half_w, WIDTH)
+                silu(0, HALF, WIDTH)
             else:
                 silu(c)
-            if c + LOOK < CHUNKS:
-                evacuate(c + LOOK, tuple(b for b in (0, 1) if 2 * (c + LOOK) + b not in EVV))
+            n = c + LOOK
+            if n < CHUNKS:
+                evacuate(nc.scalar.copy, n, (1,) if n == 3 else (0, 1))
             load_x(c)
             if c + 1 < CHUNKS:
                 layer1(c + 1)
-            if c + LOOK + 1 < CHUNKS and TPOS == 0:
-                transposes(c + LOOK + 1)
-            for k in range(FOLDS[c]):
-                fold(len(sums))
+            if c in EARLY_FOLDS:
+                fold(EARLY_FOLDS.index(c))
             if c == 0:
                 bias_ps = ps_a.tile([P, WIDTH], F32, name="bias_ps", tag="acc")
                 nc.tensor.matmul(out=bias_ps[:], lhsT=ones[:], rhs=brow[:], start=True, stop=True)
-            n = min(ADDS[c], TILES * c - state["added"])
-            stop = TILES * c
-            issue(min(stop - state["issued"], 2 - (state["issued"] - state["added"])))
-            if c in Q0F:
-                quantise0(c + LOOK)
+            issue(2, TILES * c)
+            if n == 3:
+                evacuate(nc.vector.tensor_copy, n, (0,))
             regroup(c)
-            add_some(n, 2, stop)
-            if c + LOOK + 1 < CHUNKS and TPOS == 1:
-                transposes(c + LOOK + 1)
-            if c + LOOK < CHUNKS:
-                evacuate(c + LOOK, tuple(b for b in (0, 1) if 2 * (c + LOOK) + b in EVV), True)
-                if c not in Q0F:
-                    quantise0(c + LOOK)
+            if c >= FIRST_ADDS:
+                add_up_to(state["added"] + ADDS, 2, TILES * c)
+            if n + 1 < CHUNKS:
+                transposes(n + 1)
+            if n < CHUNKS:
+                quantise0(n)
             quantise1(c)
             if c == 0:
-                if BIAS_S:
-                    nc.scalar.copy(out=b2bc[:], in_=bias_ps[:])
-                else:
-                    nc.vector.tensor_copy(out=b2bc[:], in_=bias_ps[:])
-            for k in range(CL[c]):
-                clamp(state["clamped"])
-                state["clamped"] += 1
+                nc.vector.tensor_copy(out=b2bc[:], in_=bias_ps[:])
+            if c in EARLY_CLAMPS:
+                clamp(EARLY_CLAMPS.index(c))
 
-        issue(DEEP - (state["issued"] - state["added"]))
-
-        def unload_v(c):
-            if c in UV and c in sums and c not in halves_done:
-                unload(c, True)
-                halves_done.add(c)
-
-        halves_done = set()
-        for c in range(CHUNKS):
-            if c >= state["clamped"]:
-                add_some(min(ROWS, TILES * (c + 1) + AHEAD) - state["added"], DEEP, ROWS)
-                if c < CHUNKS - 1:
-                    clamp(c, 1 if on_scalar(TILES * c) else 0)
-                state["clamped"] += 1
-            if c == CHUNKS - 1:
-                for lo in (0, 2):
-                    clamp(c, 1 if lo == 0 and on_scalar(TILES * c) else lo, lo + 2)
-                    fold(c, (lo, lo + 1))
-                    sigmoid_store(c, WIDTH * lo, WIDTH * (lo + 2))
-            if c >= VLAG:
-                unload_v(c - VLAG)
+        issue(DEEP, ROWS)
+        for c in range(CHUNKS + 1):
+            if EARLY <= c < CHUNKS:
+                add_up_to(min(ROWS, TILES * (c + 1) + 1), DEEP, ROWS)
             if c < CHUNKS - 1:
-                if c not in sums:
-                    fold(c)
+                if c >= EARLY:
+                    clamp(c)
                 sigmoid_store(c)
-            if c + 1 < CHUNKS and on_scalar(TILES * (c + 1)):
-                clamp_scalar(TILES * (c + 1))
-            if c not in UV:
-                unload(c)
-            if c >= DFROM:
-                dot_x(DOTS)
-        for c in range(CHUNKS):
-            unload_v(c)
+            elif c == CHUNKS - 1:
+                for lo in (0, 2):
+                    clamp(c, lo, lo + 2)
+                    sigmoid_store(c, lo, lo + 2)
+            if c >= 1:
+                if c - 1 >= EARLY:
+                    fold(c - 1)
+                unload(c - 1)
+
         totals = ps_a.tile([P, ROWS], F32, name="totals", tag="acc")
         for c in range(CHUNKS):
             total(c)
-        for c in range(CHUNKS):
-            dot_x(TILES * (c + 1) - state["dots"] if TILES * (c + 1) > state["dots"] else 0)
-            pair(c)
-            log_sum(c)
+        dot_x(0)
+        dot_x(1)
+        products = work.tile([P, TILES, HALF], F32, name="products", tag="clamped", bufs=3)
+        nc.vector.tensor_tensor(
+            out=products[:], in0=recon[PAIRED][:, :, :HALF], in1=recon[PAIRED][:, :, HALF:], op=ALU.mult
+        )
+        for j in range(2, ROWS):
+            dot_x(j)
+        for j in range(ROWS):
+            log_sum(j)
 
-        def by_tile(t):
-            return t.rearrange("p (c r) -> p c r", r=TILES)
-
-        def finish(rows, total_of_rows):
-            nc.vector.scalar_tensor_tensor(
-                out=rows(by_tile(part[:])),
-                in0=total_of_rows,
-                scalar=CLAMP * WIDTH,
-                in1=rows(by_tile(sum_lx[:])),
-                op0=ALU.add,
-                op1=ALU.subtract,
-            )
-
-        finish(lambda t: t[:, :, 1:], by_tile(totals[:])[:, :, 1:])
-        if SLO > 0:
-            finish(lambda t: t[:, :SLO, 0], by_tile(totals[:])[:, :SLO, 0])
-        if SLO < CHUNKS:
-            finish(lambda t: t[:, SLO:, 0], sum_rl[:, SLO:])
+        nc.vector.tensor_tensor(out=part[:], in0=totals[:], in1=sum_lx[:], op=ALU.subtract)
         nc.vector.tensor_tensor(out=bce[:], in0=part[:], in1=sum_ln[:], op=ALU.subtract)
         nc.sync.dma_start(out=out_0.rearrange("(p q) -> p q", q=ROWS), in_=bce[:])

@@ -30,7 +30,13 @@ EARLY_CLAMPS = (4, 5)
 EARLY_FOLDS = (6, 7)
 EARLY = len(EARLY_CLAMPS)
 DEEP = 4
-PAIRED = CHUNKS - 2
+PAIRED = (6,)
+BY_GPSIMD = (15, 19, 23)
+PAT = 2
+LATE_UNLOADS = 2
+LU_AT = 8
+VCOPY = 99
+GS = 0
 
 
 def tile_vae_pb_t_kernel(tc, h_dec0, x, dw1, db1, dw2, db2, out_0, out_1):
@@ -173,7 +179,9 @@ def tile_vae_pb_t_kernel(tc, h_dec0, x, dw1, db1, dw2, db2, out_0, out_1):
 
         def add_bias(j):
             c, r = divmod(j, TILES)
-            nc.vector.tensor_tensor(out=logit[c][:, r, :], in0=accs[j][:], in1=b2bc[:], op=ALU.add)
+            nc.vector.scalar_tensor_tensor(
+                out=logit[c][:, r, :], in0=accs[j][:], scalar=-1.0, in1=b2bc[:], op0=ALU.mult, op1=ALU.subtract
+            )
 
         def clamp(c, lo=0, hi=TILES):
             if c not in clamped:
@@ -182,29 +190,33 @@ def tile_vae_pb_t_kernel(tc, h_dec0, x, dw1, db1, dw2, db2, out_0, out_1):
                 else:
                     clamped[c] = work.tile([P, TILES, WIDTH], F32, name="clamped%d" % c, tag="clamped", bufs=3)
             nc.vector.tensor_scalar(
-                out=clamped[c][:, lo:hi, :], in0=logit[c][:, lo:hi, :], scalar1=CLAMP, scalar2=None, op0=ALU.max
+                out=clamped[c][:, lo:hi, :], in0=logit[c][:, lo:hi, :], scalar1=-CLAMP, scalar2=-1.0, op0=ALU.min, op1=ALU.mult
             )
 
         def fold(c):
             pool, tag = (ps_t, "xt") if c // 2 % 2 == 0 else (ps_z, "z")
             sums[c] = pool.tile([P, TILES, P], F32, name="sums%d" % c, tag=tag)
             for r in range(TILES):
-                for b in range(4):
+                terms = [clamped[c][:, r, P * b : P * (b + 1)] for b in range(4)]
+                if TILES * c + r in BY_GPSIMD:
+                    terms += [logit[c][:, r, P * b : P * (b + 1)] for b in range(4)]
+                for n, term in enumerate(terms):
                     nc.tensor.matmul(
-                        out=sums[c][:, r, :],
-                        lhsT=clamped[c][:, r, P * b : P * (b + 1)],
-                        rhs=ident[:],
-                        is_transpose=True,
-                        start=b == 0,
-                        stop=b == 3,
+                        out=sums[c][:, r, :], lhsT=term, rhs=ident[:], is_transpose=True, start=n == 0, stop=n == len(terms) - 1
                     )
 
-        def unload(c):
+        def multiply_x(j):
+            c, r = divmod(j, TILES)
+            nc.gpsimd.tensor_tensor(
+                out=logit[c][:, r, :], in0=logit[c][:, r, :], in1=xs[c][:, WIDTH * r : WIDTH * (r + 1)], op=ALU.mult
+            )
+
+        def unload(copy, c):
             if c % 2 == 0:
                 tag = "hs" if c < 4 else "g1"
                 halves[c] = work.tile([P, 2, TILES, P], F32, name="halves%d" % c, tag=tag, align_bytes=64)
                 halves[c + 1] = halves[c]
-            nc.scalar.copy(out=halves[c][:, c % 2, :, :], in_=sums[c][:])
+            copy(out=halves[c][:, c % 2, :, :], in_=sums[c][:])
 
         def total(c):
             for r in range(TILES):
@@ -225,8 +237,8 @@ def tile_vae_pb_t_kernel(tc, h_dec0, x, dw1, db1, dw2, db2, out_0, out_1):
 
         def log_sum(j):
             c, r = divmod(j, TILES)
-            source = products[:, r, :] if c == PAIRED else recon[c][:, r, :]
-            width = HALF if c == PAIRED else WIDTH
+            source = products[:, PAIRED.index(c), r, :] if c in PAIRED else recon[c][:, r, :]
+            width = HALF if c in PAIRED else WIDTH
             nc.scalar.activation(
                 out=unread[:, j % 2, :width], in_=source, func=ACT.Ln, accum_out=sum_ln[:, j : j + 1]
             )
@@ -249,6 +261,7 @@ def tile_vae_pb_t_kernel(tc, h_dec0, x, dw1, db1, dw2, db2, out_0, out_1):
         nc.gpsimd.memset(warm[:], 0.0)
         nc.scalar.activation(out=warm[:], in_=warm[:], func=ACT.Silu)
         nc.vector.memset(onesf[:], 1.0)
+        nc.vector.memset(sum_lx[:], 0.0)
         make_identity(nc, ident[:])
         nc.gpsimd.memset(ones[:], 1.0)
         h0[0] = io.tile([P, CW], BF16, name="h0_0", tag="io")
@@ -285,9 +298,9 @@ def tile_vae_pb_t_kernel(tc, h_dec0, x, dw1, db1, dw2, db2, out_0, out_1):
         group1(nc.vector.tensor_copy, 1)
         quant1(0)
         quantise0(0, 0, HALF)
-        group1(nc.scalar.copy, 2)
+        group1(nc.scalar.copy if GS else nc.vector.tensor_copy, 2)
         quant1(1)
-        group1(nc.scalar.copy, 3)
+        group1(nc.scalar.copy if GS else nc.vector.tensor_copy, 3)
         quant1(2)
         quant1(3)
         transposes(0, (1,))
@@ -328,7 +341,7 @@ def tile_vae_pb_t_kernel(tc, h_dec0, x, dw1, db1, dw2, db2, out_0, out_1):
                 silu(c)
             n = c + LOOK
             if n < CHUNKS:
-                evacuate(nc.scalar.copy, n, (1,) if n == 3 else (0, 1))
+                evacuate(nc.scalar.copy, n, (1,) if n == VCOPY else (0, 1))
             load_x(c)
             if c + 1 < CHUNKS:
                 layer1(c + 1)
@@ -338,7 +351,7 @@ def tile_vae_pb_t_kernel(tc, h_dec0, x, dw1, db1, dw2, db2, out_0, out_1):
                 bias_ps = ps_a.tile([P, WIDTH], F32, name="bias_ps", tag="acc")
                 nc.tensor.matmul(out=bias_ps[:], lhsT=ones[:], rhs=brow[:], start=True, stop=True)
             issue(2, TILES * c)
-            if n == 3:
+            if n == VCOPY:
                 evacuate(nc.vector.tensor_copy, n, (0,))
             regroup(c)
             if c >= FIRST_ADDS:
@@ -360,6 +373,9 @@ def tile_vae_pb_t_kernel(tc, h_dec0, x, dw1, db1, dw2, db2, out_0, out_1):
             if c < CHUNKS - 1:
                 if c >= EARLY:
                     clamp(c)
+                    for j in range(TILES * c, TILES * (c + 1)):
+                        if j in BY_GPSIMD:
+                            multiply_x(j)
                 sigmoid_store(c)
             elif c == CHUNKS - 1:
                 for lo in (0, 2):
@@ -368,22 +384,31 @@ def tile_vae_pb_t_kernel(tc, h_dec0, x, dw1, db1, dw2, db2, out_0, out_1):
             if c >= 1:
                 if c - 1 >= EARLY:
                     fold(c - 1)
-                unload(c - 1)
+                if c - 1 < CHUNKS - LATE_UNLOADS:
+                    unload(nc.scalar.copy, c - 1)
 
         totals = ps_a.tile([P, ROWS], F32, name="totals", tag="acc")
-        for c in range(CHUNKS):
+        for c in range(CHUNKS - LATE_UNLOADS):
             total(c)
-        dot_x(0)
-        dot_x(1)
-        products = work.tile([P, TILES, HALF], F32, name="products", tag="clamped", bufs=3)
-        nc.vector.tensor_tensor(
-            out=products[:], in0=recon[PAIRED][:, :, :HALF], in1=recon[PAIRED][:, :, HALF:], op=ALU.mult
-        )
-        for j in range(2, ROWS):
+        lu = []
+        dots = [j for j in range(ROWS) if j not in BY_GPSIMD]
+        for j in dots[:PAT]:
             dot_x(j)
+        products = work.tile([P, 2, TILES, HALF], F32, name="products", tag="clamped", bufs=3)
+        for n, c in enumerate(PAIRED):
+            nc.vector.tensor_tensor(
+                out=products[:, n, :, :], in0=recon[c][:, :, :HALF], in1=recon[c][:, :, HALF:], op=ALU.mult
+            )
+        for j in dots[PAT:]:
+            dot_x(j)
+            if j >= LU_AT and not lu:
+                lu.append(j)
+                for c in range(CHUNKS - LATE_UNLOADS, CHUNKS):
+                    unload(nc.vector.tensor_copy, c)
+                    total(c)
         for j in range(ROWS):
             log_sum(j)
 
-        nc.vector.tensor_tensor(out=part[:], in0=totals[:], in1=sum_lx[:], op=ALU.subtract)
+        nc.vector.tensor_tensor(out=part[:], in0=totals[:], in1=sum_lx[:], op=ALU.add)
         nc.vector.tensor_tensor(out=bce[:], in0=part[:], in1=sum_ln[:], op=ALU.subtract)
         nc.sync.dma_start(out=out_0.rearrange("(p q) -> p q", q=ROWS), in_=bce[:])

@@ -22,22 +22,18 @@ CW = TILES * WIDTH
 HALF = WIDTH // 2
 CLAMP = -40.0
 LOOK = 2
-GROUPED_BY_GPSIMD = 208
-LAP = 8
 ADDS = 3
 FIRST_ADDS = 2
-EARLY_CLAMPS = (4, 5)
-EARLY_FOLDS = (6, 7)
-EARLY = len(EARLY_CLAMPS)
+GROUPED_BY_GPSIMD = 224
+LAP = 8
+EARLY = 2
+SCALAR_CLAMP_ROUND = 6
+CLAMP_ROUND = 5
+FOLD_ROUND = 7
 DEEP = 4
-PAIRED = (6,)
-BY_GPSIMD = (15, 19, 23)
-PAT = 2
-LATE_UNLOADS = 2
-LU_AT = 8
-VCOPY = 99
-GS = 0
-
+BY_GPSIMD = [TILES * c + TILES - 1 for c in range(EARLY + 1, CHUNKS - 1)]
+LATE_SUMS = 4
+PAIRED = CHUNKS - 2
 
 def tile_vae_pb_t_kernel(tc, h_dec0, x, dw1, db1, dw2, db2, out_0, out_1):
     nc = tc.nc
@@ -67,12 +63,15 @@ def tile_vae_pb_t_kernel(tc, h_dec0, x, dw1, db1, dw2, db2, out_0, out_1):
         brow = const.tile([P, WIDTH], BF16, name="brow")
         sum_lx = const.tile([P, ROWS], F32, name="sum_lx")
         sum_ln = const.tile([P, ROWS], F32, name="sum_ln")
+        sum_shifted = const.tile([P, TILES], F32, name="sum_shifted")
         onesf = const.tile([P, 1], F32, name="onesf")
+        up = const.tile([P, 1], F32, name="up")
+        down = const.tile([P, 1], F32, name="down")
         warm = const.tile([P, 1], F32, name="warm")
         part = const.tile([P, ROWS], F32, name="part")
         bce = const.tile([P, ROWS], F32, name="bce")
         unread = const.tile([P, 2, WIDTH], BF16, name="unread")
-        logit = [const.tile([P, TILES, WIDTH], F32, name="logit%d" % c) for c in range(CHUNKS)]
+        minus_l = [const.tile([P, TILES, WIDTH], F32, name="minus_l%d" % c) for c in range(CHUNKS)]
         recon = [const.tile([P, TILES, WIDTH], F32, name="recon%d" % c) for c in range(CHUNKS)]
 
         h0, xs, xts, g0, c0, s0 = {}, {}, {}, {}, {}, {}
@@ -180,7 +179,7 @@ def tile_vae_pb_t_kernel(tc, h_dec0, x, dw1, db1, dw2, db2, out_0, out_1):
         def add_bias(j):
             c, r = divmod(j, TILES)
             nc.vector.scalar_tensor_tensor(
-                out=logit[c][:, r, :], in0=accs[j][:], scalar=-1.0, in1=b2bc[:], op0=ALU.mult, op1=ALU.subtract
+                out=minus_l[c][:, r, :], in0=accs[j][:], scalar=-1.0, in1=b2bc[:], op0=ALU.mult, op1=ALU.subtract
             )
 
         def clamp(c, lo=0, hi=TILES):
@@ -190,46 +189,63 @@ def tile_vae_pb_t_kernel(tc, h_dec0, x, dw1, db1, dw2, db2, out_0, out_1):
                 else:
                     clamped[c] = work.tile([P, TILES, WIDTH], F32, name="clamped%d" % c, tag="clamped", bufs=3)
             nc.vector.tensor_scalar(
-                out=clamped[c][:, lo:hi, :], in0=logit[c][:, lo:hi, :], scalar1=-CLAMP, scalar2=-1.0, op0=ALU.min, op1=ALU.mult
+                out=clamped[c][:, lo:hi, :],
+                in0=minus_l[c][:, lo:hi, :],
+                scalar1=-CLAMP,
+                scalar2=-1.0,
+                op0=ALU.min,
+                op1=ALU.mult,
             )
+
+        def clamp_on_scalar():
+            clamped[0] = recon[0]
+            for r in range(TILES):
+                nc.scalar.activation(
+                    out=recon[0][:, r, :],
+                    in_=minus_l[0][:, r, :],
+                    func=ACT.Relu,
+                    bias=up[:],
+                    scale=-1.0,
+                    accum_out=sum_shifted[:, r : r + 1],
+                )
 
         def fold(c):
             pool, tag = (ps_t, "xt") if c // 2 % 2 == 0 else (ps_z, "z")
             sums[c] = pool.tile([P, TILES, P], F32, name="sums%d" % c, tag=tag)
             for r in range(TILES):
-                terms = [clamped[c][:, r, P * b : P * (b + 1)] for b in range(4)]
-                if TILES * c + r in BY_GPSIMD:
-                    terms += [logit[c][:, r, P * b : P * (b + 1)] for b in range(4)]
-                for n, term in enumerate(terms):
+                terms = [clamped[c]] if TILES * c + r not in BY_GPSIMD else [clamped[c], minus_l[c]]
+                blocks = [term[:, r, P * b : P * (b + 1)] for term in terms for b in range(4)]
+                for n, block in enumerate(blocks):
                     nc.tensor.matmul(
-                        out=sums[c][:, r, :], lhsT=term, rhs=ident[:], is_transpose=True, start=n == 0, stop=n == len(terms) - 1
+                        out=sums[c][:, r, :],
+                        lhsT=block,
+                        rhs=ident[:],
+                        is_transpose=True,
+                        start=n == 0,
+                        stop=n == len(blocks) - 1,
                     )
 
-        def multiply_x(j):
-            c, r = divmod(j, TILES)
-            nc.gpsimd.tensor_tensor(
-                out=logit[c][:, r, :], in0=logit[c][:, r, :], in1=xs[c][:, WIDTH * r : WIDTH * (r + 1)], op=ALU.mult
-            )
-
         def unload(copy, c):
-            if c % 2 == 0:
+            if c // 2 not in halves:
                 tag = "hs" if c < 4 else "g1"
-                halves[c] = work.tile([P, 2, TILES, P], F32, name="halves%d" % c, tag=tag, align_bytes=64)
-                halves[c + 1] = halves[c]
-            copy(out=halves[c][:, c % 2, :, :], in_=sums[c][:])
+                halves[c // 2] = work.tile([P, 2, TILES, P], F32, name="halves%d" % c, tag=tag, align_bytes=64)
+            copy(out=halves[c // 2][:, c % 2, :, :], in_=sums[c][:])
 
         def total(c):
             for r in range(TILES):
                 nc.tensor.matmul(
                     out=totals[:, TILES * c + r : TILES * c + r + 1],
-                    lhsT=halves[c][:, c % 2, r, :],
+                    lhsT=halves[c // 2][:, c % 2, r, :],
                     rhs=onesf[:],
                     start=True,
                     stop=True,
                 )
 
         def sigmoid_store(c, lo=0, hi=TILES):
-            nc.scalar.activation(out=recon[c][:, lo:hi, :], in_=clamped[c][:, lo:hi, :], func=ACT.Sigmoid)
+            shift = down[:] if c == 0 else 0.0
+            nc.scalar.activation(
+                out=recon[c][:, lo:hi, :], in_=clamped[c][:, lo:hi, :], func=ACT.Sigmoid, bias=shift, scale=1.0
+            )
             nc.sync.dma_start(
                 out=o_rows[:, CW * c + WIDTH * lo : CW * c + WIDTH * hi],
                 in_=recon[c][:, lo:hi, :].rearrange("p r k -> p (r k)"),
@@ -237,17 +253,23 @@ def tile_vae_pb_t_kernel(tc, h_dec0, x, dw1, db1, dw2, db2, out_0, out_1):
 
         def log_sum(j):
             c, r = divmod(j, TILES)
-            source = products[:, PAIRED.index(c), r, :] if c in PAIRED else recon[c][:, r, :]
-            width = HALF if c in PAIRED else WIDTH
+            source = products[:, r, :] if c == PAIRED else recon[c][:, r, :]
+            width = HALF if c == PAIRED else WIDTH
             nc.scalar.activation(
                 out=unread[:, j % 2, :width], in_=source, func=ACT.Ln, accum_out=sum_ln[:, j : j + 1]
+            )
+
+        def multiply_x(j):
+            c, r = divmod(j, TILES)
+            nc.gpsimd.tensor_tensor(
+                out=minus_l[c][:, r, :], in0=minus_l[c][:, r, :], in1=xs[c][:, WIDTH * r : WIDTH * (r + 1)], op=ALU.mult
             )
 
         def dot_x(j):
             c, r = divmod(j, TILES)
             nc.vector.scalar_tensor_tensor(
-                out=logit[c][:, r, :],
-                in0=logit[c][:, r, :],
+                out=minus_l[c][:, r, :],
+                in0=minus_l[c][:, r, :],
                 scalar=1.0,
                 in1=xs[c][:, WIDTH * r : WIDTH * (r + 1)],
                 op0=ALU.mult,
@@ -262,6 +284,8 @@ def tile_vae_pb_t_kernel(tc, h_dec0, x, dw1, db1, dw2, db2, out_0, out_1):
         nc.scalar.activation(out=warm[:], in_=warm[:], func=ACT.Silu)
         nc.vector.memset(onesf[:], 1.0)
         nc.vector.memset(sum_lx[:], 0.0)
+        nc.vector.memset(up[:], -CLAMP)
+        nc.vector.memset(down[:], CLAMP)
         make_identity(nc, ident[:])
         nc.gpsimd.memset(ones[:], 1.0)
         h0[0] = io.tile([P, CW], BF16, name="h0_0", tag="io")
@@ -283,8 +307,8 @@ def tile_vae_pb_t_kernel(tc, h_dec0, x, dw1, db1, dw2, db2, out_0, out_1):
         grouped1 = wg1[:].rearrange("p (s m t) -> p s m t", s=4, m=P, t=4)
         rows1 = raw1[:].rearrange("p (t m s) -> p s m t", t=4, m=P, s=4)
 
-        def group1(copy, s):
-            copy(out=grouped1[:, s, :, :], in_=rows1[:, s, :, :])
+        def group1(s):
+            nc.vector.tensor_copy(out=grouped1[:, s, :, :], in_=rows1[:, s, :, :])
 
         def quant1(s):
             cols = slice(P * s, P * (s + 1))
@@ -294,13 +318,13 @@ def tile_vae_pb_t_kernel(tc, h_dec0, x, dw1, db1, dw2, db2, out_0, out_1):
 
         transposes(0, (0,))
         evacuate(nc.scalar.copy, 0, (0,))
-        group1(nc.vector.tensor_copy, 0)
-        group1(nc.vector.tensor_copy, 1)
+        group1(0)
+        group1(1)
         quant1(0)
         quantise0(0, 0, HALF)
-        group1(nc.scalar.copy if GS else nc.vector.tensor_copy, 2)
+        group1(2)
         quant1(1)
-        group1(nc.scalar.copy if GS else nc.vector.tensor_copy, 3)
+        group1(3)
         quant1(2)
         quant1(3)
         transposes(0, (1,))
@@ -341,18 +365,18 @@ def tile_vae_pb_t_kernel(tc, h_dec0, x, dw1, db1, dw2, db2, out_0, out_1):
                 silu(c)
             n = c + LOOK
             if n < CHUNKS:
-                evacuate(nc.scalar.copy, n, (1,) if n == VCOPY else (0, 1))
+                evacuate(nc.scalar.copy, n)
             load_x(c)
             if c + 1 < CHUNKS:
                 layer1(c + 1)
-            if c in EARLY_FOLDS:
-                fold(EARLY_FOLDS.index(c))
+            if c == SCALAR_CLAMP_ROUND:
+                clamp_on_scalar()
+            if c == FOLD_ROUND:
+                fold(1)
             if c == 0:
                 bias_ps = ps_a.tile([P, WIDTH], F32, name="bias_ps", tag="acc")
                 nc.tensor.matmul(out=bias_ps[:], lhsT=ones[:], rhs=brow[:], start=True, stop=True)
             issue(2, TILES * c)
-            if n == VCOPY:
-                evacuate(nc.vector.tensor_copy, n, (0,))
             regroup(c)
             if c >= FIRST_ADDS:
                 add_up_to(state["added"] + ADDS, 2, TILES * c)
@@ -363,8 +387,8 @@ def tile_vae_pb_t_kernel(tc, h_dec0, x, dw1, db1, dw2, db2, out_0, out_1):
             quantise1(c)
             if c == 0:
                 nc.vector.tensor_copy(out=b2bc[:], in_=bias_ps[:])
-            if c in EARLY_CLAMPS:
-                clamp(EARLY_CLAMPS.index(c))
+            if c == CLAMP_ROUND:
+                clamp(1)
 
         issue(DEEP, ROWS)
         for c in range(CHUNKS + 1):
@@ -373,42 +397,48 @@ def tile_vae_pb_t_kernel(tc, h_dec0, x, dw1, db1, dw2, db2, out_0, out_1):
             if c < CHUNKS - 1:
                 if c >= EARLY:
                     clamp(c)
-                    for j in range(TILES * c, TILES * (c + 1)):
-                        if j in BY_GPSIMD:
-                            multiply_x(j)
+                for j in range(TILES * c, TILES * (c + 1)):
+                    if j in BY_GPSIMD:
+                        multiply_x(j)
                 sigmoid_store(c)
             elif c == CHUNKS - 1:
                 for lo in (0, 2):
                     clamp(c, lo, lo + 2)
                     sigmoid_store(c, lo, lo + 2)
-            if c >= 1:
-                if c - 1 >= EARLY:
-                    fold(c - 1)
-                if c - 1 < CHUNKS - LATE_UNLOADS:
-                    unload(nc.scalar.copy, c - 1)
+            if c - 1 >= EARLY:
+                fold(c - 1)
+            if 1 <= c - 1 < CHUNKS - LATE_SUMS:
+                unload(nc.scalar.copy, c - 1)
 
         totals = ps_a.tile([P, ROWS], F32, name="totals", tag="acc")
-        for c in range(CHUNKS - LATE_UNLOADS):
+        for c in range(1, CHUNKS - LATE_SUMS):
             total(c)
-        lu = []
-        dots = [j for j in range(ROWS) if j not in BY_GPSIMD]
-        for j in dots[:PAT]:
-            dot_x(j)
-        products = work.tile([P, 2, TILES, HALF], F32, name="products", tag="clamped", bufs=3)
-        for n, c in enumerate(PAIRED):
-            nc.vector.tensor_tensor(
-                out=products[:, n, :, :], in0=recon[c][:, :, :HALF], in1=recon[c][:, :, HALF:], op=ALU.mult
-            )
-        for j in dots[PAT:]:
-            dot_x(j)
-            if j >= LU_AT and not lu:
-                lu.append(j)
-                for c in range(CHUNKS - LATE_UNLOADS, CHUNKS):
+        dot_x(0)
+        dot_x(1)
+        products = work.tile([P, TILES, HALF], F32, name="products", tag="clamped", bufs=3)
+        nc.vector.tensor_tensor(
+            out=products[:], in0=recon[PAIRED][:, :, :HALF], in1=recon[PAIRED][:, :, HALF:], op=ALU.mult
+        )
+        for j in range(2, ROWS):
+            if j not in BY_GPSIMD:
+                dot_x(j)
+            if j == 8:
+                for c in range(CHUNKS - LATE_SUMS, CHUNKS):
                     unload(nc.vector.tensor_copy, c)
                     total(c)
         for j in range(ROWS):
             log_sum(j)
 
-        nc.vector.tensor_tensor(out=part[:], in0=totals[:], in1=sum_lx[:], op=ALU.add)
+        nc.vector.tensor_tensor(
+            out=part[:, TILES:], in0=totals[:, TILES:], in1=sum_lx[:, TILES:], op=ALU.add
+        )
+        nc.vector.scalar_tensor_tensor(
+            out=part[:, :TILES],
+            in0=sum_shifted[:],
+            scalar=CLAMP * WIDTH,
+            in1=sum_lx[:, :TILES],
+            op0=ALU.add,
+            op1=ALU.add,
+        )
         nc.vector.tensor_tensor(out=bce[:], in0=part[:], in1=sum_ln[:], op=ALU.subtract)
         nc.sync.dma_start(out=out_0.rearrange("(p q) -> p q", q=ROWS), in_=bce[:])

from contextlib import ExitStack

import concourse.mybir as mybir
from concourse.masks import make_identity

F32 = mybir.dt.float32
BF16 = mybir.dt.bfloat16
U32 = mybir.dt.uint32
U8 = mybir.dt.uint8
FP8X4 = mybir.dt.float8_e4m3fn_x4
ACT = mybir.ActivationFunctionType
ALU = mybir.AluOpType

P = 128
BATCH = 4096
WIDTH = 512
FLOPS = 2 * 2 * BATCH * WIDTH * WIDTH
ROWS = BATCH // P
TILES = 4
CHUNKS = ROWS // TILES
CW = TILES * WIDTH
HALF = WIDTH // 2
CLAMP = -40.0
LOOK = 2
ADDS = 3
FIRST_ADDS = 2
GROUPED_BY_GPSIMD = 224
LAP = 8
EARLY = 2
SCALAR_CLAMP_ROUND = 6
CLAMP_ROUND = 5
FOLD_ROUND = 7
DEEP = 4
BY_GPSIMD = [TILES * c + TILES - 1 for c in range(EARLY + 1, CHUNKS - 1)]
LATE_SUMS = 4
PAIRED = CHUNKS - 2

def tile_vae_pb_t_kernel(tc, h_dec0, x, dw1, db1, dw2, db2, out_0, out_1):
    nc = tc.nc
    h_rows = h_dec0.rearrange("(p q) k -> p (q k)", q=ROWS)
    x_rows = x.rearrange("(p q) k -> p (q k)", q=ROWS)
    o_rows = out_1.rearrange("(p q) k -> p (q k)", q=ROWS)

    with ExitStack() as ctx:
        const = ctx.enter_context(tc.tile_pool(name="const", bufs=1))
        io = ctx.enter_context(tc.tile_pool(name="io", bufs=CHUNKS))
        work = ctx.enter_context(tc.tile_pool(name="work", bufs=2))
        ps_t = ctx.enter_context(tc.psum_pool(name="ps_t", bufs=2))
        ps_y = ctx.enter_context(tc.psum_pool(name="ps_y", bufs=2))
        ps_z = ctx.enter_context(tc.psum_pool(name="ps_z", bufs=2))
        ps_a = ctx.enter_context(tc.psum_pool(name="ps_a", bufs=2))
        ctx.enter_context(tc.manual_schedule())

        ident = const.tile([P, P], F32, name="ident")
        w1c = const.tile([P, WIDTH], U32, name="w1c", align_bytes=64)
        w1s = const.tile([P, WIDTH], U8, name="w1s", align_bytes=64)
        w2c = const.tile([P, WIDTH], U32, name="w2c", align_bytes=64)
        w2s = const.tile([P, WIDTH], U8, name="w2s", align_bytes=64)
        b1r = const.tile([P, 4], BF16, name="b1r")
        b1f = const.tile([P, 4], F32, name="b1f")
        b2bc = const.tile([P, WIDTH], F32, name="b2bc")
        ones = const.tile([P, P], BF16, name="ones")
        brow = const.tile([P, WIDTH], BF16, name="brow")
        sum_lx = const.tile([P, ROWS], F32, name="sum_lx")
        sum_ln = const.tile([P, ROWS], F32, name="sum_ln")
        sum_shifted = const.tile([P, TILES], F32, name="sum_shifted")
        onesf = const.tile([P, 1], F32, name="onesf")
        up = const.tile([P, 1], F32, name="up")
        down = const.tile([P, 1], F32, name="down")
        warm = const.tile([P, 1], F32, name="warm")
        part = const.tile([P, ROWS], F32, name="part")
        bce = const.tile([P, ROWS], F32, name="bce")
        unread = const.tile([P, 2, WIDTH], BF16, name="unread")
        minus_l = [const.tile([P, TILES, WIDTH], F32, name="minus_l%d" % c) for c in range(CHUNKS)]
        recon = [const.tile([P, TILES, WIDTH], F32, name="recon%d" % c) for c in range(CHUNKS)]

        h0, xs, xts, g0, c0, s0 = {}, {}, {}, {}, {}, {}
        zs, hs, g1, c1, s1 = {}, {}, {}, {}, {}
        accs, clamped, sums, halves = {}, {}, {}, {}

        def load_h(c):
            h0[c] = io.tile([P, CW], BF16, name="h0_%d" % c, tag="io")
            nc.sync.dma_start(out=h0[c][:], in_=h_rows[:, CW * c : CW * (c + 1)])

        def load_x(c):
            xs[c] = io.tile([P, CW], BF16, name="x_%d" % c, tag="io")
            nc.sync.dma_start(out=xs[c][:], in_=x_rows[:, CW * c : CW * (c + 1)])

        def transposes(c, bs=(0, 1), pool=ps_t, tag="xt"):
            words = h0[c][:].bitcast(F32)
            for b in bs:
                xt = pool.tile([P, 2, 256], F32, name="xt%d_%d" % (c, b), tag=tag)
                for r2 in range(2):
                    for u in range(2):
                        lo = 256 * (2 * b + r2) + P * u
                        nc.tensor.transpose(xt[:, u, P * r2 : P * (r2 + 1)], words[:, lo : lo + P], ident[:])
                xts[(c, b)] = xt

        def evacuate(copy, c, bs=(0, 1)):
            if c not in g0:
                g0[c] = work.tile([P, CW], BF16, name="g0_%d" % c, tag="g0", bufs=LOOK, align_bytes=64)
            words = g0[c][:].bitcast(F32).rearrange("p (w u) -> p w u", u=2)
            for b in bs:
                copy(out=words[:, 256 * b : 256 * (b + 1), :], in_=xts[(c, b)][:].rearrange("p u w -> p w u"))

        def quantise0(c, lo=0, hi=WIDTH):
            if lo == 0:
                c0[c] = work.tile([P, WIDTH], U32, name="c0_%d" % c, tag="c0", bufs=LOOK, align_bytes=64)
                s0[c] = work.tile([P, WIDTH], U8, name="s0_%d" % c, tag="s0", bufs=LOOK, align_bytes=64)
            nc.vector.quantize_mx(
                out=c0[c][:, lo:hi].bitcast(FP8X4), scales=s0[c][:, lo:hi], in_=g0[c][:, 4 * lo : 4 * hi]
            )

        def layer1(c, lo=0, hi=WIDTH):
            per_bank = WIDTH // (hi - lo)
            for t in range(4):
                if t % per_bank == 0:
                    pool, tag = (ps_y, "y") if t < 2 else (ps_z, "z")
                    z = pool.tile([P, per_bank, hi - lo], F32, name="z%d_%d_%d" % (c, lo, t), tag=tag)
                zs[(c, lo, t)] = z[:, t % per_bank, :]
                nc.tensor.matmul_mx(
                    out=zs[(c, lo, t)],
                    lhsT=w1c[:, P * t : P * (t + 1)].bitcast(FP8X4),
                    lhsT_scale=w1s[:, P * t : P * (t + 1)],
                    rhs=c0[c][:, lo:hi].bitcast(FP8X4),
                    rhs_scale=s0[c][:, lo:hi],
                    start=True,
                    stop=True,
                )

        def silu(c, lo=0, hi=WIDTH):
            if lo == 0:
                hs[c] = work.tile([P, 4, WIDTH], BF16, name="hs%d" % c, tag="hs", align_bytes=64)
            for t in (1, 0, 3, 2):
                nc.scalar.activation(
                    out=hs[c][:, t, lo:hi], in_=zs[(c, lo, t)], func=ACT.Silu, bias=b1f[:, t : t + 1], scale=1.0
                )

        def regroup(c):
            g1[c] = work.tile([P, WIDTH, 4], BF16, name="g1_%d" % c, tag="g1", align_bytes=64)
            cut = WIDTH - GROUPED_BY_GPSIMD if c >= FIRST_ADDS else WIDTH
            own = min(WIDTH, cut + LAP)
            nc.vector.tensor_copy(
                out=g1[c][:, :own, :].rearrange("p (c i) t -> p c t i", i=4),
                in_=hs[c][:, :, :own].rearrange("p t (c i) -> p c t i", i=4),
            )
            if cut < WIDTH:
                nc.gpsimd.tensor_scalar(
                    out=g1[c][:, cut:, :],
                    in0=hs[c][:, :, cut:].rearrange("p t n -> p n t"),
                    scalar1=1.0,
                    scalar2=0.0,
                    op0=ALU.mult,
                    op1=ALU.add,
                )

        def quantise1(c):
            c1[c] = work.tile([P, WIDTH], U32, name="c1_%d" % c, tag="c1", bufs=4, align_bytes=64)
            s1[c] = work.tile([P, WIDTH], U8, name="s1_%d" % c, tag="s1", bufs=4, align_bytes=64)
            nc.vector.quantize_mx(
                out=c1[c][:].bitcast(FP8X4), scales=s1[c][:], in_=g1[c][:].rearrange("p w t -> p (w t)")
            )

        def layer2(j):
            c, r = divmod(j, TILES)
            pool, tag = (ps_y, "y") if j in in_y else (ps_a, "acc")
            acc = pool.tile([P, WIDTH], F32, name="acc%d" % j, tag=tag)
            nc.tensor.matmul_mx(
                out=acc[:],
                lhsT=c1[c][:, P * r : P * (r + 1)].bitcast(FP8X4),
                lhsT_scale=s1[c][:, P * r : P * (r + 1)],
                rhs=w2c[:].bitcast(FP8X4),
                rhs_scale=w2s[:],
                start=True,
                stop=True,
            )
            accs[j] = acc

        def add_bias(j):
            c, r = divmod(j, TILES)
            nc.vector.scalar_tensor_tensor(
                out=minus_l[c][:, r, :], in0=accs[j][:], scalar=-1.0, in1=b2bc[:], op0=ALU.mult, op1=ALU.subtract
            )

        def clamp(c, lo=0, hi=TILES):
            if c not in clamped:
                if c < EARLY:
                    clamped[c] = recon[c]
                else:
                    clamped[c] = work.tile([P, TILES, WIDTH], F32, name="clamped%d" % c, tag="clamped", bufs=3)
            nc.vector.tensor_scalar(
                out=clamped[c][:, lo:hi, :],
                in0=minus_l[c][:, lo:hi, :],
                scalar1=-CLAMP,
                scalar2=-1.0,
                op0=ALU.min,
                op1=ALU.mult,
            )

        def clamp_on_scalar():
            clamped[0] = recon[0]
            for r in range(TILES):
                nc.scalar.activation(
                    out=recon[0][:, r, :],
                    in_=minus_l[0][:, r, :],
                    func=ACT.Relu,
                    bias=up[:],
                    scale=-1.0,
                    accum_out=sum_shifted[:, r : r + 1],
                )

        def fold(c):
            pool, tag = (ps_t, "xt") if c // 2 % 2 == 0 else (ps_z, "z")
            sums[c] = pool.tile([P, TILES, P], F32, name="sums%d" % c, tag=tag)
            for r in range(TILES):
                terms = [clamped[c]] if TILES * c + r not in BY_GPSIMD else [clamped[c], minus_l[c]]
                blocks = [term[:, r, P * b : P * (b + 1)] for term in terms for b in range(4)]
                for n, block in enumerate(blocks):
                    nc.tensor.matmul(
                        out=sums[c][:, r, :],
                        lhsT=block,
                        rhs=ident[:],
                        is_transpose=True,
                        start=n == 0,
                        stop=n == len(blocks) - 1,
                    )

        def unload(copy, c):
            if c // 2 not in halves:
                tag = "hs" if c < 4 else "g1"
                halves[c // 2] = work.tile([P, 2, TILES, P], F32, name="halves%d" % c, tag=tag, align_bytes=64)
            copy(out=halves[c // 2][:, c % 2, :, :], in_=sums[c][:])

        def total(c):
            for r in range(TILES):
                nc.tensor.matmul(
                    out=totals[:, TILES * c + r : TILES * c + r + 1],
                    lhsT=halves[c // 2][:, c % 2, r, :],
                    rhs=onesf[:],
                    start=True,
                    stop=True,
                )

        def sigmoid_store(c, lo=0, hi=TILES):
            shift = down[:] if c == 0 else 0.0
            nc.scalar.activation(
                out=recon[c][:, lo:hi, :], in_=clamped[c][:, lo:hi, :], func=ACT.Sigmoid, bias=shift, scale=1.0
            )
            nc.sync.dma_start(
                out=o_rows[:, CW * c + WIDTH * lo : CW * c + WIDTH * hi],
                in_=recon[c][:, lo:hi, :].rearrange("p r k -> p (r k)"),
            )

        def log_sum(j):
            c, r = divmod(j, TILES)
            source = products[:, r, :] if c == PAIRED else recon[c][:, r, :]
            width = HALF if c == PAIRED else WIDTH
            nc.scalar.activation(
                out=unread[:, j % 2, :width], in_=source, func=ACT.Ln, accum_out=sum_ln[:, j : j + 1]
            )

        def multiply_x(j):
            c, r = divmod(j, TILES)
            nc.gpsimd.tensor_tensor(
                out=minus_l[c][:, r, :], in0=minus_l[c][:, r, :], in1=xs[c][:, WIDTH * r : WIDTH * (r + 1)], op=ALU.mult
            )

        def dot_x(j):
            c, r = divmod(j, TILES)
            nc.vector.scalar_tensor_tensor(
                out=minus_l[c][:, r, :],
                in0=minus_l[c][:, r, :],
                scalar=1.0,
                in1=xs[c][:, WIDTH * r : WIDTH * (r + 1)],
                op0=ALU.mult,
                op1=ALU.mult,
                accum_out=sum_lx[:, j : j + 1],
            )

        nc.scalar.dma_start(out=b1r[:], in_=db1.rearrange("(p t) -> p t", t=4))
        nc.vector.memset(brow[:], 0.0)
        nc.scalar.dma_start(out=brow[0:1, :], in_=db2.rearrange("(o n) -> o n", o=1))
        nc.gpsimd.memset(warm[:], 0.0)
        nc.scalar.activation(out=warm[:], in_=warm[:], func=ACT.Silu)
        nc.vector.memset(onesf[:], 1.0)
        nc.vector.memset(sum_lx[:], 0.0)
        nc.vector.memset(up[:], -CLAMP)
        nc.vector.memset(down[:], CLAMP)
        make_identity(nc, ident[:])
        nc.gpsimd.memset(ones[:], 1.0)
        h0[0] = io.tile([P, CW], BF16, name="h0_0", tag="io")
        nc.sync.dma_start(out=h0[0][:, : CW // 2], in_=h_rows[:, : CW // 2])
        raw1 = work.tile([P, CW], BF16, name="raw1", tag="hs", align_bytes=64)
        nc.sync.dma_start(
            out=raw1[:].rearrange("p (u f) -> p u f", u=2),
            in_=dw1.rearrange("(u p e) n -> p u (e n)", u=2, p=P, e=2),
        )
        nc.sync.dma_start(out=h0[0][:, CW // 2 :], in_=h_rows[:, CW // 2 : CW])
        load_h(1)
        raw2 = work.tile([P, CW], BF16, name="raw2", tag="hs", align_bytes=64)
        nc.sync.dma_start(out=raw2[:], in_=dw2.rearrange("(p t) n -> p (t n)", t=4))
        for c in range(2, CHUNKS):
            load_h(c)

        nc.vector.tensor_copy(out=b1f[:], in_=b1r[:])
        wg1 = work.tile([P, CW], BF16, name="wg1", tag="g1", align_bytes=64)
        grouped1 = wg1[:].rearrange("p (s m t) -> p s m t", s=4, m=P, t=4)
        rows1 = raw1[:].rearrange("p (t m s) -> p s m t", t=4, m=P, s=4)

        def group1(s):
            nc.vector.tensor_copy(out=grouped1[:, s, :, :], in_=rows1[:, s, :, :])

        def quant1(s):
            cols = slice(P * s, P * (s + 1))
            nc.vector.quantize_mx(
                out=w1c[:, cols].bitcast(FP8X4), scales=w1s[:, cols], in_=wg1[:, 4 * P * s : 4 * P * (s + 1)]
            )

        transposes(0, (0,))
        evacuate(nc.scalar.copy, 0, (0,))
        group1(0)
        group1(1)
        quant1(0)
        quantise0(0, 0, HALF)
        group1(2)
        quant1(1)
        group1(3)
        quant1(2)
        quant1(3)
        transposes(0, (1,))
        evacuate(nc.scalar.copy, 0, (1,))
        transposes(1, pool=ps_a, tag="acc")
        layer1(0, 0, HALF)
        silu(0, 0, HALF)
        quantise0(0, HALF, WIDTH)
        layer1(0, HALF, WIDTH)
        evacuate(nc.vector.tensor_copy, 1)
        quantise0(1)
        wg2 = work.tile([P, CW], BF16, name="wg2", tag="g1", align_bytes=64)
        nc.vector.tensor_copy(
            out=wg2[:].rearrange("p (c i t) -> p c t i", i=4, t=4), in_=raw2[:].rearrange("p (t c i) -> p c t i", t=4, i=4)
        )
        nc.vector.quantize_mx(out=w2c[:].bitcast(FP8X4), scales=w2s[:], in_=wg2[:])
        transposes(LOOK)

        late = ADDS * (CHUNKS - FIRST_ADDS) + 2
        in_y = [j for j in range(late, ROWS) if (j - late) // 2 % 2 == 0]
        state = {"added": 0, "issued": 0}

        def issue(depth, ready):
            while state["issued"] < min(ready, state["added"] + depth):
                layer2(state["issued"])
                state["issued"] += 1

        def add_up_to(end, depth, ready):
            while state["added"] < end:
                add_bias(state["added"])
                state["added"] += 1
                issue(depth, ready)

        for c in range(CHUNKS):
            if c == 0:
                silu(0, HALF, WIDTH)
            else:
                silu(c)
            n = c + LOOK
            if n < CHUNKS:
                evacuate(nc.scalar.copy, n)
            load_x(c)
            if c + 1 < CHUNKS:
                layer1(c + 1)
            if c == SCALAR_CLAMP_ROUND:
                clamp_on_scalar()
            if c == FOLD_ROUND:
                fold(1)
            if c == 0:
                bias_ps = ps_a.tile([P, WIDTH], F32, name="bias_ps", tag="acc")
                nc.tensor.matmul(out=bias_ps[:], lhsT=ones[:], rhs=brow[:], start=True, stop=True)
            issue(2, TILES * c)
            regroup(c)
            if c >= FIRST_ADDS:
                add_up_to(state["added"] + ADDS, 2, TILES * c)
            if n + 1 < CHUNKS:
                transposes(n + 1)
            if n < CHUNKS:
                quantise0(n)
            quantise1(c)
            if c == 0:
                nc.vector.tensor_copy(out=b2bc[:], in_=bias_ps[:])
            if c == CLAMP_ROUND:
                clamp(1)

        issue(DEEP, ROWS)
        for c in range(CHUNKS + 1):
            if EARLY <= c < CHUNKS:
                add_up_to(min(ROWS, TILES * (c + 1) + 1), DEEP, ROWS)
            if c < CHUNKS - 1:
                if c >= EARLY:
                    clamp(c)
                for j in range(TILES * c, TILES * (c + 1)):
                    if j in BY_GPSIMD:
                        multiply_x(j)
                sigmoid_store(c)
            elif c == CHUNKS - 1:
                for lo in (0, 2):
                    clamp(c, lo, lo + 2)
                    sigmoid_store(c, lo, lo + 2)
            if c - 1 >= EARLY:
                fold(c - 1)
            if 1 <= c - 1 < CHUNKS - LATE_SUMS:
                unload(nc.scalar.copy, c - 1)

        totals = ps_a.tile([P, ROWS], F32, name="totals", tag="acc")
        for c in range(1, CHUNKS - LATE_SUMS):
            total(c)
        dot_x(0)
        dot_x(1)
        products = work.tile([P, TILES, HALF], F32, name="products", tag="clamped", bufs=3)
        nc.vector.tensor_tensor(
            out=products[:], in0=recon[PAIRED][:, :, :HALF], in1=recon[PAIRED][:, :, HALF:], op=ALU.mult
        )
        for j in range(2, ROWS):
            if j not in BY_GPSIMD:
                dot_x(j)
            if j == 8:
                for c in range(CHUNKS - LATE_SUMS, CHUNKS):
                    unload(nc.vector.tensor_copy, c)
                    total(c)
        for j in range(ROWS):
            log_sum(j)

        nc.vector.tensor_tensor(
            out=part[:, TILES:], in0=totals[:, TILES:], in1=sum_lx[:, TILES:], op=ALU.add
        )
        nc.vector.scalar_tensor_tensor(
            out=part[:, :TILES],
            in0=sum_shifted[:],
            scalar=CLAMP * WIDTH,
            in1=sum_lx[:, :TILES],
            op0=ALU.add,
            op1=ALU.add,
        )
        nc.vector.tensor_tensor(out=bce[:], in0=part[:], in1=sum_ln[:], op=ALU.subtract)
        nc.sync.dma_start(out=out_0.rearrange("(p q) -> p q", q=ROWS), in_=bce[:])
